import numpy as np
import ml_dtypes


def mxq(x, axis, fmt="e4m3"):
    dtype, down = {"e4m3": (ml_dtypes.float8_e4m3fn, 7), "e5m2": (ml_dtypes.float8_e5m2, 14)}[fmt]
    v = np.moveaxis(np.asarray(x, np.float32).astype(ml_dtypes.bfloat16).astype(np.float64), axis, -1)
    blocks = v.reshape(v.shape[:-1] + (-1, 32))
    amax = np.abs(blocks).max(-1, keepdims=True)
    byte = np.maximum(np.where(amax > 0, np.frexp(amax)[1] - 1 + 127, 0) - down, 1)
    scale = np.exp2(byte - 127.0)
    codes = (blocks / scale).astype(np.float32).astype(dtype).astype(np.float64)
    return np.moveaxis((codes * scale).reshape(v.shape), -1, axis)


WIDE = False


def mx_kscale(k):
    if not WIDE:
        return np.ones(k)
    levels = np.array([10, -10, 5, -5, 0])
    a = np.random.permutation(np.resize(levels, k // 512 * 4)).reshape(k // 512, 4)
    idx = np.arange(k)
    return np.exp2(a[idx // 512, idx % 128 // 32])


BF16 = ml_dtypes.bfloat16


def bf(x):
    return np.asarray(x, np.float32).astype(BF16)


def f64(x):
    return np.asarray(x).astype(np.float64)


B, I, R, O = 128, 8, 64, 2
K = I * R
N = R * O


def setup_inputs():
    s = mx_kscale(K).reshape(I, R)
    v = mx_kscale(K)[:R]
    return {"t_first": bf(np.random.standard_normal((B, I, I, I, R, O)) * s[None, :, None, None, :, None]),
            "mid_core0": bf(np.random.standard_normal((I, R, R, O)) / np.sqrt(K) / s[:, :, None, None] * v[None, None, :, None]),
            "mid_core1": bf(np.random.standard_normal((I, R, R, O)) / np.sqrt(K) / v[None, :, None, None])}


def reference(t_first, mid_core0, mid_core1):
    a = f64(t_first).transpose(0, 2, 3, 5, 1, 4).reshape(B * I * I * O, K)
    t = mxq(a, 1, "e4m3") @ mxq(f64(mid_core0).reshape(K, N), 0, "e4m3")
    t = t.reshape(B, I, I, O, R, O)
    a = t.transpose(0, 2, 3, 5, 1, 4).reshape(B * I * O * O, K)
    t = mxq(a, 1, "e4m3") @ mxq(f64(mid_core1).reshape(K, N), 0, "e4m3")
    return t.reshape(B, I, O, O, R, O)

@@ -1,0 +1,224 @@
+from contextlib import ExitStack
+
+import concourse.mybir as mybir
+from concourse.masks import make_identity
+
+BF16 = mybir.dt.bfloat16
+F32 = mybir.dt.float32
+U32 = mybir.dt.uint32
+U8 = mybir.dt.uint8
+FP8X4 = mybir.dt.float8_e4m3fn_x4
+
+P = 128
+PACK = 4
+B, I, R, O = 128, 8, 64, 2
+HALVES = P // R
+ROW = I * R * O
+B_CHUNK = P // PACK
+N_BQ = B // B_CHUNK
+GROUPS = I // PACK
+Z_PAIRS = I // HALVES
+N_OUT = R * O
+BANK = 512
+
+N_CHUNKS = N_BQ * GROUPS
+N_UNITS = N_CHUNKS * GROUPS
+LOADS_AHEAD = 6
+EARLY_BANKS = 2
+
+FLOPS = 2 * (B * I * I * O) * (I * R) * N_OUT + 2 * (B * I * O * O) * (I * R) * N_OUT
+
+
+def tile_mpolinear2_pa_t_kernel(tc, t_first, mid_core0, mid_core1, out):
+    nc = tc.nc
+    with ExitStack() as ctx:
+        consts = ctx.enter_context(tc.tile_pool(name="consts", bufs=1))
+        raw_pool = ctx.enter_context(tc.tile_pool(name="raw_pool", bufs=LOADS_AHEAD))
+        grouped_pool = ctx.enter_context(tc.tile_pool(name="grouped_pool", bufs=3))
+        work = ctx.enter_context(tc.tile_pool(name="work", bufs=2))
+        psum_t = ctx.enter_context(tc.psum_pool(name="psum_t", bufs=Z_PAIRS))
+        psum_1 = ctx.enter_context(tc.psum_pool(name="psum_1", bufs=HALVES))
+        psum_2 = ctx.enter_context(tc.psum_pool(name="psum_2", bufs=2))
+        ctx.enter_context(tc.manual_schedule())
+
+        raw, banks, grouped, codes, scales = {}, {}, {}, {}, {}
+        accs, mids, mid_codes, mid_scales, accs2, results = {}, {}, {}, {}, {}, {}
+
+        def load(unit):
+            if unit >= N_UNITS:
+                return
+            chunk, g = divmod(unit, GROUPS)
+            bq, yg = divmod(chunk, GROUPS)
+            raw[unit] = raw_pool.tile([P, PACK, ROW], BF16, name="raw")
+            for y in range(PACK):
+                nc.sync.dma_start(
+                    out=raw[unit][y:P:PACK],
+                    in_=t_first[bq * B_CHUNK : (bq + 1) * B_CHUNK, g:I:GROUPS, yg * PACK + y].rearrange(
+                        "b x z r o -> b x (z r o)"
+                    ),
+                )
+
+        def transpose_bank(unit, zh):
+            if unit >= N_UNITS:
+                return
+            bank = psum_t.tile([P, PACK, P], F32, name="bank")
+            words = raw[unit][:].bitcast(F32)
+            for t in range(PACK):
+                nc.tensor.transpose(bank[:, t, :], words[:, t, zh * P : (zh + 1) * P], ident[:])
+            banks[unit, zh] = bank
+
+        def empty_bank(unit, zh):
+            if zh == 0:
+                grouped[unit] = grouped_pool.tile([P, O, Z_PAIRS, P, PACK], BF16, name="grouped", align_bytes=64)
+            halves = banks[unit, zh][:].bitcast(BF16).rearrange("k t (c o) -> k o c t", o=O)
+            if zh == Z_PAIRS - 1:
+                nc.vector.tensor_copy(out=grouped[unit][:, :, zh], in_=halves)
+            else:
+                nc.scalar.copy(out=grouped[unit][:, :, zh], in_=halves)
+
+        def quantise_unit(unit):
+            if not 0 <= unit < N_UNITS:
+                return
+            chunk, g = divmod(unit, GROUPS)
+            if g == 0:
+                codes[chunk] = work.tile([P, GROUPS, O, BANK], U32, name="codes", align_bytes=64)
+                scales[chunk] = work.tile([P, GROUPS, O, BANK], U8, name="scales", align_bytes=64)
+            for o in range(O):
+                nc.vector.quantize_mx(
+                    out=codes[chunk][:, g, o].bitcast(FP8X4),
+                    scales=scales[chunk][:, g, o],
+                    in_=grouped[unit][:, o].rearrange("k z c t -> k (z c t)"),
+                )
+
+        def first_contraction(pair):
+            if not 0 <= pair < N_CHUNKS * O:
+                return
+            chunk, o = divmod(pair, O)
+            for h in range(HALVES):
+                acc = psum_1.tile([P, BANK], F32, name="acc")
+                for g in range(GROUPS):
+                    nc.tensor.matmul_mx(
+                        out=acc[:],
+                        lhsT=core0_codes[:, g, h].bitcast(FP8X4),
+                        lhsT_scale=core0_scales[:, g, h],
+                        rhs=codes[chunk][:, g, o].bitcast(FP8X4),
+                        rhs_scale=scales[chunk][:, g, o],
+                        start=(g == 0),
+                        stop=(g == GROUPS - 1),
+                    )
+                accs[pair, h] = acc
+
+        def round_mid(pair):
+            if not 0 <= pair < N_CHUNKS * O:
+                return
+            chunk, o = divmod(pair, O)
+            if o == 0:
+                mids[chunk] = work.tile([P, O, HALVES, BANK], BF16, name="mid", align_bytes=64)
+            for h in range(HALVES):
+                nc.vector.tensor_copy(out=mids[chunk][:, o, h], in_=accs[pair, h][:])
+
+        def quantise_mid(chunk):
+            bq, yg = divmod(chunk, GROUPS)
+            if yg == 0:
+                mid_codes[bq] = work.tile([P, GROUPS, O, HALVES, P], U32, name="mid_codes", align_bytes=64)
+                mid_scales[bq] = work.tile([P, GROUPS, O, HALVES, P], U8, name="mid_scales", align_bytes=64)
+            nc.vector.quantize_mx(
+                out=mid_codes[bq][:, yg].rearrange("k o h c -> k (o h c)").bitcast(FP8X4),
+                scales=mid_scales[bq][:, yg].rearrange("k o h c -> k (o h c)"),
+                in_=mids[chunk][:].rearrange("k o h n -> k (o h n)"),
+            )
+
+        def second_contraction(group):
+            if not 0 <= group < N_BQ * HALVES * O:
+                return
+            bq, h, o = group // (HALVES * O), group // O % HALVES, group % O
+            if o == 0:
+                accs2[bq, h] = psum_2.tile([P, O, HALVES * N_OUT], F32, name="acc2")
+            for yg in range(GROUPS):
+                nc.tensor.matmul_mx(
+                    out=accs2[bq, h][:, o],
+                    lhsT=mid_codes[bq][:, yg, o, h].bitcast(FP8X4),
+                    lhsT_scale=mid_scales[bq][:, yg, o, h],
+                    rhs=core1_codes[:, yg].bitcast(FP8X4),
+                    rhs_scale=core1_scales[:, yg],
+                    start=(yg == 0),
+                    stop=(yg == GROUPS - 1),
+                )
+
+        def finish(group):
+            if not 0 <= group < N_BQ * HALVES * O or group % O != O - 1:
+                return
+            bq, h = group // (HALVES * O), group // O % HALVES
+            if h == 0:
+                results[bq] = work.tile([P, HALVES, O, HALVES * N_OUT], F32, name="result")
+            nc.scalar.copy(out=results[bq][:, h], in_=accs2[bq, h][:])
+            if h == HALVES - 1:
+                for zh in range(Z_PAIRS):
+                    nc.scalar.dma_start(
+                        out=out[bq * B_CHUNK : (bq + 1) * B_CHUNK, HALVES * zh : HALVES * (zh + 1)].rearrange(
+                            "b z o p u q -> b (z o p u q)"
+                        ),
+                        in_=results[bq][zh * B_CHUNK : (zh + 1) * B_CHUNK].rearrange("k h o n -> k (h o n)"),
+                    )
+
+        for unit in range(LOADS_AHEAD):
+            load(unit)
+
+        ident = consts.tile([P, P], F32, name="ident")
+        make_identity(nc, ident[:])
+
+        core0_raw = consts.tile([P, I, N_OUT], BF16, name="core0_raw")
+        core1_raw = consts.tile([P, I, N_OUT], BF16, name="core1_raw")
+        for h in range(HALVES):
+            rows = slice(h * R, (h + 1) * R)
+            nc.scalar.dma_start(out=core0_raw[rows], in_=mid_core0.rearrange("x r s p -> r x (s p)"))
+            nc.scalar.dma_start(out=core1_raw[rows], in_=mid_core1.rearrange("y s u q -> s y (u q)"))
+        core0_grouped = consts.tile([P, GROUPS, HALVES, N_OUT, PACK], BF16, name="core0_grouped", align_bytes=64)
+        core1_grouped = consts.tile([P, GROUPS, HALVES, N_OUT, PACK], BF16, name="core1_grouped", align_bytes=64)
+        core0_codes = consts.tile([P, GROUPS, HALVES, N_OUT], U32, name="core0_codes", align_bytes=64)
+        core0_scales = consts.tile([P, GROUPS, HALVES, N_OUT], U8, name="core0_scales", align_bytes=64)
+        core1_codes = consts.tile([P, GROUPS, HALVES * N_OUT], U32, name="core1_codes", align_bytes=64)
+        core1_scales = consts.tile([P, GROUPS, HALVES * N_OUT], U8, name="core1_scales", align_bytes=64)
+        nc.vector.memset(core0_grouped[:], 0.0)
+        nc.vector.memset(core1_grouped[:], 0.0)
+        for h in range(HALVES):
+            rows = slice(h * R, (h + 1) * R)
+            for g in range(GROUPS):
+                nc.vector.tensor_copy(
+                    out=core0_grouped[rows, g, h].rearrange("k (p s) t -> k p s t", p=O),
+                    in_=core0_raw[rows, g:I:GROUPS, :].rearrange("k t (s p) -> k p s t", p=O),
+                )
+            nc.vector.tensor_copy(
+                out=core1_grouped[rows, :, h],
+                in_=core1_raw[rows].rearrange("k (g t) n -> k g n t", t=PACK),
+            )
+        nc.vector.quantize_mx(
+            out=core0_codes[:].rearrange("k g h m -> k (g h m)").bitcast(FP8X4),
+            scales=core0_scales[:].rearrange("k g h m -> k (g h m)"),
+            in_=core0_grouped[:].rearrange("k g h m t -> k (g h m t)"),
+        )
+        nc.vector.quantize_mx(
+            out=core1_codes[:].rearrange("k g n -> k (g n)").bitcast(FP8X4),
+            scales=core1_scales[:].rearrange("k g n -> k (g n)"),
+            in_=core1_grouped[:].rearrange("k g h n t -> k (g h n t)"),
+        )
+
+        for zh in range(Z_PAIRS):
+            transpose_bank(0, zh)
+        for step in range(N_UNITS + 9):
+            if step < N_UNITS:
+                for zh in range(Z_PAIRS):
+                    empty_bank(step, zh)
+                    if zh < EARLY_BANKS:
+                        transpose_bank(step + 1, zh)
+            round_mid(step - 3)
+            quantise_unit(step - 1)
+            if step >= 4 and step % GROUPS == 0 and step // GROUPS - 2 < N_CHUNKS:
+                quantise_mid(step // GROUPS - 2)
+            first_contraction(step - 2)
+            second_contraction(step - 7)
+            if step < N_UNITS:
+                for zh in range(EARLY_BANKS, Z_PAIRS):
+                    transpose_bank(step + 1, zh)
+                load(step + LOADS_AHEAD)
+            finish(step - 8)

@@ -23,8 +23,16 @@ BANK = 512
 
 N_CHUNKS = N_BQ * GROUPS
 N_UNITS = N_CHUNKS * GROUPS
+N_PAIRS = N_CHUNKS * O
+N_FINAL = N_BQ * HALVES * O
 LOADS_AHEAD = 6
-EARLY_BANKS = 2
+
+QUANTISE_LAG = 1
+FIRST_LAG = 3
+ROUND_LAG = FIRST_LAG + 1
+SECOND_LAG = 2 * GROUPS + ROUND_LAG
+FINISH_LAG = SECOND_LAG + 1
+N_STEPS = N_UNITS + FINISH_LAG
 
 FLOPS = 2 * (B * I * I * O) * (I * R) * N_OUT + 2 * (B * I * O * O) * (I * R) * N_OUT
 
@@ -90,34 +98,35 @@ def tile_mpolinear2_pa_t_kernel(tc, t_first, mid_core0, mid_core1, out):
                     in_=grouped[unit][:, o].rearrange("k z c t -> k (z c t)"),
                 )
 
-        def first_contraction(pair):
-            if not 0 <= pair < N_CHUNKS * O:
+        def first_contraction(pair, h):
+            if not 0 <= pair < N_PAIRS:
                 return
             chunk, o = divmod(pair, O)
-            for h in range(HALVES):
-                acc = psum_1.tile([P, BANK], F32, name="acc")
-                for g in range(GROUPS):
-                    nc.tensor.matmul_mx(
-                        out=acc[:],
-                        lhsT=core0_codes[:, g, h].bitcast(FP8X4),
-                        lhsT_scale=core0_scales[:, g, h],
-                        rhs=codes[chunk][:, g, o].bitcast(FP8X4),
-                        rhs_scale=scales[chunk][:, g, o],
-                        start=(g == 0),
-                        stop=(g == GROUPS - 1),
-                    )
-                accs[pair, h] = acc
+            acc = psum_1.tile([P, BANK], F32, name="acc")
+            for g in range(GROUPS):
+                nc.tensor.matmul_mx(
+                    out=acc[:],
+                    lhsT=core0_codes[:, g, h].bitcast(FP8X4),
+                    lhsT_scale=core0_scales[:, g, h],
+                    rhs=codes[chunk][:, g, o].bitcast(FP8X4),
+                    rhs_scale=scales[chunk][:, g, o],
+                    start=(g == 0),
+                    stop=(g == GROUPS - 1),
+                )
+            accs[pair, h] = acc
 
-        def round_mid(pair):
-            if not 0 <= pair < N_CHUNKS * O:
+        def round_mid(pair, h):
+            if not 0 <= pair < N_PAIRS:
                 return
             chunk, o = divmod(pair, O)
-            if o == 0:
+            if o == 0 and h == 0:
                 mids[chunk] = work.tile([P, O, HALVES, BANK], BF16, name="mid", align_bytes=64)
-            for h in range(HALVES):
-                nc.vector.tensor_copy(out=mids[chunk][:, o, h], in_=accs[pair, h][:])
+            nc.vector.tensor_copy(out=mids[chunk][:, o, h], in_=accs[pair, h][:])
 
-        def quantise_mid(chunk):
+        def quantise_mid(pair):
+            if not 0 <= pair < N_PAIRS or pair % O != O - 1:
+                return
+            chunk = pair // O
             bq, yg = divmod(chunk, GROUPS)
             if yg == 0:
                 mid_codes[bq] = work.tile([P, GROUPS, O, HALVES, P], U32, name="mid_codes", align_bytes=64)
@@ -129,7 +138,7 @@ def tile_mpolinear2_pa_t_kernel(tc, t_first, mid_core0, mid_core1, out):
             )
 
         def second_contraction(group):
-            if not 0 <= group < N_BQ * HALVES * O:
+            if not 0 <= group < N_FINAL:
                 return
             bq, h, o = group // (HALVES * O), group // O % HALVES, group % O
             if o == 0:
@@ -146,7 +155,7 @@ def tile_mpolinear2_pa_t_kernel(tc, t_first, mid_core0, mid_core1, out):
                 )
 
         def finish(group):
-            if not 0 <= group < N_BQ * HALVES * O or group % O != O - 1:
+            if not 0 <= group < N_FINAL or group % O != O - 1:
                 return
             bq, h = group // (HALVES * O), group // O % HALVES
             if h == 0:
@@ -203,22 +212,24 @@ def tile_mpolinear2_pa_t_kernel(tc, t_first, mid_core0, mid_core1, out):
             in_=core1_grouped[:].rearrange("k g h n t -> k (g h n t)"),
         )
 
-        for zh in range(Z_PAIRS):
+        def turn_over(unit, zh):
+            if unit < N_UNITS:
+                empty_bank(unit, zh)
+                transpose_bank(unit + 1, zh)
+
+        for zh in (0, 3, 1, 2):
             transpose_bank(0, zh)
-        for step in range(N_UNITS + 9):
-            if step < N_UNITS:
-                for zh in range(Z_PAIRS):
-                    empty_bank(step, zh)
-                    if zh < EARLY_BANKS:
-                        transpose_bank(step + 1, zh)
-            round_mid(step - 3)
-            quantise_unit(step - 1)
-            if step >= 4 and step % GROUPS == 0 and step // GROUPS - 2 < N_CHUNKS:
-                quantise_mid(step // GROUPS - 2)
-            first_contraction(step - 2)
-            second_contraction(step - 7)
-            if step < N_UNITS:
-                for zh in range(EARLY_BANKS, Z_PAIRS):
-                    transpose_bank(step + 1, zh)
-                load(step + LOADS_AHEAD)
-            finish(step - 8)
+        for step in range(N_STEPS):
+            round_mid(step - ROUND_LAG, 0)
+            first_contraction(step - FIRST_LAG, 0)
+            turn_over(step, 0)
+            turn_over(step, 3)
+            turn_over(step, 1)
+            round_mid(step - ROUND_LAG, 1)
+            first_contraction(step - FIRST_LAG, 1)
+            second_contraction(step - SECOND_LAG)
+            turn_over(step, 2)
+            quantise_unit(step - QUANTISE_LAG)
+            quantise_mid(step - ROUND_LAG)
+            finish(step - FINISH_LAG)
+            load(step + LOADS_AHEAD)

@@ -13,24 +13,22 @@ P = 128
 PACK = 4
 B, I, R, O = 128, 8, 64, 2
 HALVES = P // R
-ROW = I * R * O
-B_CHUNK = P // PACK
-N_BQ = B // B_CHUNK
 GROUPS = I // PACK
-Z_PAIRS = I // HALVES
 N_OUT = R * O
 BANK = 512
 
-N_CHUNKS = N_BQ * GROUPS
-N_UNITS = N_CHUNKS * GROUPS
-N_PAIRS = N_CHUNKS * O
-N_FINAL = N_BQ * HALVES * O
+ZQ, ZL = 2, 2
+B_CHUNK = P // PACK
+N_BQ = B // B_CHUNK
+N_UNITS = N_BQ * GROUPS * ZQ
+N_FINAL = N_BQ * ZQ * HALVES
 LOADS_AHEAD = 6
 
 QUANTISE_LAG = 1
-FIRST_LAG = 3
-ROUND_LAG = FIRST_LAG + 1
-SECOND_LAG = 2 * GROUPS + ROUND_LAG
+FIRST_LAG = 2
+ROUND_LAG = 3
+MID_LAG = 4
+SECOND_LAG = GROUPS * ZQ - ZQ + MID_LAG
 FINISH_LAG = SECOND_LAG + 1
 N_STEPS = N_UNITS + FINISH_LAG
 
@@ -42,112 +40,111 @@ def tile_mpolinear2_pa_t_kernel(tc, t_first, mid_core0, mid_core1, out):
     with ExitStack() as ctx:
         consts = ctx.enter_context(tc.tile_pool(name="consts", bufs=1))
         raw_pool = ctx.enter_context(tc.tile_pool(name="raw_pool", bufs=LOADS_AHEAD))
-        grouped_pool = ctx.enter_context(tc.tile_pool(name="grouped_pool", bufs=3))
-        work = ctx.enter_context(tc.tile_pool(name="work", bufs=2))
-        psum_t = ctx.enter_context(tc.psum_pool(name="psum_t", bufs=Z_PAIRS))
+        work = ctx.enter_context(tc.tile_pool(name="work", bufs=3))
+        psum_t = ctx.enter_context(tc.psum_pool(name="psum_t", bufs=GROUPS * ZL))
         psum_1 = ctx.enter_context(tc.psum_pool(name="psum_1", bufs=HALVES))
         psum_2 = ctx.enter_context(tc.psum_pool(name="psum_2", bufs=2))
         ctx.enter_context(tc.manual_schedule())
 
         raw, banks, grouped, codes, scales = {}, {}, {}, {}, {}
-        accs, mids, mid_codes, mid_scales, accs2, results = {}, {}, {}, {}, {}, {}
+        accs, mids, mid_codes, mid_scales, accs2 = {}, {}, {}, {}, {}
+
+        def split_unit(unit):
+            return unit // (GROUPS * ZQ), unit // ZQ % GROUPS, unit % ZQ
 
         def load(unit):
             if unit >= N_UNITS:
                 return
-            chunk, g = divmod(unit, GROUPS)
-            bq, yg = divmod(chunk, GROUPS)
-            raw[unit] = raw_pool.tile([P, PACK, ROW], BF16, name="raw")
+            bq, yg, zq = split_unit(unit)
+            raw[unit] = raw_pool.tile([P, I, ZL * HALVES * R * O], BF16, name="raw")
             for y in range(PACK):
                 nc.sync.dma_start(
                     out=raw[unit][y:P:PACK],
-                    in_=t_first[bq * B_CHUNK : (bq + 1) * B_CHUNK, g:I:GROUPS, yg * PACK + y].rearrange(
-                        "b x z r o -> b x (z r o)"
-                    ),
+                    in_=t_first[
+                        bq * B_CHUNK : (bq + 1) * B_CHUNK, :, yg * PACK + y, zq * ZL * HALVES : (zq + 1) * ZL * HALVES
+                    ].rearrange("b x z r o -> b x (z r o)"),
                 )
 
-        def transpose_bank(unit, zh):
+        def transpose_bank(unit, g, zl):
             if unit >= N_UNITS:
                 return
             bank = psum_t.tile([P, PACK, P], F32, name="bank")
             words = raw[unit][:].bitcast(F32)
             for t in range(PACK):
-                nc.tensor.transpose(bank[:, t, :], words[:, t, zh * P : (zh + 1) * P], ident[:])
-            banks[unit, zh] = bank
+                nc.tensor.transpose(bank[:, t, :], words[:, g + GROUPS * t, zl * P : (zl + 1) * P], ident[:])
+            banks[unit, g, zl] = bank
 
-        def empty_bank(unit, zh):
-            if zh == 0:
-                grouped[unit] = grouped_pool.tile([P, O, Z_PAIRS, P, PACK], BF16, name="grouped", align_bytes=64)
-            halves = banks[unit, zh][:].bitcast(BF16).rearrange("k t (c o) -> k o c t", o=O)
-            if zh == Z_PAIRS - 1:
-                nc.vector.tensor_copy(out=grouped[unit][:, :, zh], in_=halves)
+        def turn_over(unit, g, zl):
+            if unit >= N_UNITS:
+                return
+            if g == 0 and zl == 0:
+                grouped[unit] = work.tile([P, GROUPS, O, ZL, P, PACK], BF16, name="grouped", align_bytes=64)
+            halves = banks[unit, g, zl][:].bitcast(BF16).rearrange("k t (c o) -> k o c t", o=O)
+            if zl == 0:
+                nc.scalar.copy(out=grouped[unit][:, g, :, zl], in_=halves)
             else:
-                nc.scalar.copy(out=grouped[unit][:, :, zh], in_=halves)
+                nc.vector.tensor_copy(out=grouped[unit][:, g, :, zl], in_=halves)
+            transpose_bank(unit + 1, g, zl)
 
-        def quantise_unit(unit):
+        def quantise_unit(unit, g):
             if not 0 <= unit < N_UNITS:
                 return
-            chunk, g = divmod(unit, GROUPS)
             if g == 0:
-                codes[chunk] = work.tile([P, GROUPS, O, BANK], U32, name="codes", align_bytes=64)
-                scales[chunk] = work.tile([P, GROUPS, O, BANK], U8, name="scales", align_bytes=64)
-            for o in range(O):
-                nc.vector.quantize_mx(
-                    out=codes[chunk][:, g, o].bitcast(FP8X4),
-                    scales=scales[chunk][:, g, o],
-                    in_=grouped[unit][:, o].rearrange("k z c t -> k (z c t)"),
-                )
+                codes[unit] = work.tile([P, GROUPS, BANK], U32, name="codes", align_bytes=64)
+                scales[unit] = work.tile([P, GROUPS, BANK], U8, name="scales", align_bytes=64)
+            nc.vector.quantize_mx(
+                out=codes[unit][:, g].bitcast(FP8X4),
+                scales=scales[unit][:, g],
+                in_=grouped[unit][:, g].rearrange("k o z c t -> k (o z c t)"),
+            )
 
-        def first_contraction(pair, h):
-            if not 0 <= pair < N_PAIRS:
+        def first_contraction(unit, h):
+            if not 0 <= unit < N_UNITS:
                 return
-            chunk, o = divmod(pair, O)
             acc = psum_1.tile([P, BANK], F32, name="acc")
             for g in range(GROUPS):
                 nc.tensor.matmul_mx(
                     out=acc[:],
                     lhsT=core0_codes[:, g, h].bitcast(FP8X4),
                     lhsT_scale=core0_scales[:, g, h],
-                    rhs=codes[chunk][:, g, o].bitcast(FP8X4),
-                    rhs_scale=scales[chunk][:, g, o],
+                    rhs=codes[unit][:, g].bitcast(FP8X4),
+                    rhs_scale=scales[unit][:, g],
                     start=(g == 0),
                     stop=(g == GROUPS - 1),
                 )
-            accs[pair, h] = acc
+            accs[unit, h] = acc
 
-        def round_mid(pair, h):
-            if not 0 <= pair < N_PAIRS:
+        def round_mid(unit, h):
+            if not 0 <= unit < N_UNITS:
                 return
-            chunk, o = divmod(pair, O)
-            if o == 0 and h == 0:
-                mids[chunk] = work.tile([P, O, HALVES, BANK], BF16, name="mid", align_bytes=64)
-            nc.vector.tensor_copy(out=mids[chunk][:, o, h], in_=accs[pair, h][:])
+            if h == 0:
+                mids[unit] = work.tile([P, HALVES, BANK], BF16, name="mid", align_bytes=64)
+            nc.scalar.copy(out=mids[unit][:, h], in_=accs[unit, h][:])
 
-        def quantise_mid(pair):
-            if not 0 <= pair < N_PAIRS or pair % O != O - 1:
+        def quantise_mid(unit):
+            if not 0 <= unit < N_UNITS:
                 return
-            chunk = pair // O
-            bq, yg = divmod(chunk, GROUPS)
-            if yg == 0:
-                mid_codes[bq] = work.tile([P, GROUPS, O, HALVES, P], U32, name="mid_codes", align_bytes=64)
-                mid_scales[bq] = work.tile([P, GROUPS, O, HALVES, P], U8, name="mid_scales", align_bytes=64)
+            bq, yg, zq = split_unit(unit)
+            if yg == 0 and zq == 0:
+                mid_codes[bq] = work.tile([P, GROUPS, ZQ, HALVES, P], U32, name="mid_codes", align_bytes=64)
+                mid_scales[bq] = work.tile([P, GROUPS, ZQ, HALVES, P], U8, name="mid_scales", align_bytes=64)
             nc.vector.quantize_mx(
-                out=mid_codes[bq][:, yg].rearrange("k o h c -> k (o h c)").bitcast(FP8X4),
-                scales=mid_scales[bq][:, yg].rearrange("k o h c -> k (o h c)"),
-                in_=mids[chunk][:].rearrange("k o h n -> k (o h n)"),
+                out=mid_codes[bq][:, yg, zq].rearrange("k h c -> k (h c)").bitcast(FP8X4),
+                scales=mid_scales[bq][:, yg, zq].rearrange("k h c -> k (h c)"),
+                in_=mids[unit][:].rearrange("k h n -> k (h n)"),
             )
 
         def second_contraction(group):
             if not 0 <= group < N_FINAL:
                 return
-            bq, h, o = group // (HALVES * O), group // O % HALVES, group % O
-            if o == 0:
-                accs2[bq, h] = psum_2.tile([P, O, HALVES * N_OUT], F32, name="acc2")
+            bq, zq, h = group // (ZQ * HALVES), group // HALVES % ZQ, group % HALVES
+            if h == 0:
+                accs2[bq, zq] = psum_2.tile([P, HALVES, HALVES * N_OUT], F32, name="acc2")
             for yg in range(GROUPS):
                 nc.tensor.matmul_mx(
-                    out=accs2[bq, h][:, o],
-                    lhsT=mid_codes[bq][:, yg, o, h].bitcast(FP8X4),
-                    lhsT_scale=mid_scales[bq][:, yg, o, h],
+                    out=accs2[bq, zq][:, h],
+                    lhsT=mid_codes[bq][:, yg, zq, h].bitcast(FP8X4),
+                    lhsT_scale=mid_scales[bq][:, yg, zq, h],
                     rhs=core1_codes[:, yg].bitcast(FP8X4),
                     rhs_scale=core1_scales[:, yg],
                     start=(yg == 0),
@@ -155,19 +152,20 @@ def tile_mpolinear2_pa_t_kernel(tc, t_first, mid_core0, mid_core1, out):
                 )
 
         def finish(group):
-            if not 0 <= group < N_FINAL or group % O != O - 1:
+            if not 0 <= group < N_FINAL or group % HALVES != HALVES - 1:
                 return
-            bq, h = group // (HALVES * O), group // O % HALVES
-            if h == 0:
-                results[bq] = work.tile([P, HALVES, O, HALVES * N_OUT], F32, name="result")
-            nc.scalar.copy(out=results[bq][:, h], in_=accs2[bq, h][:])
-            if h == HALVES - 1:
-                for zh in range(Z_PAIRS):
-                    nc.scalar.dma_start(
-                        out=out[bq * B_CHUNK : (bq + 1) * B_CHUNK, HALVES * zh : HALVES * (zh + 1)].rearrange(
-                            "b z o p u q -> b (z o p u q)"
+            bq, zq = group // (ZQ * HALVES), group // HALVES % ZQ
+            result = work.tile([P, HALVES, HALVES * N_OUT], F32, name="result")
+            nc.scalar.copy(out=result[:], in_=accs2[bq, zq][:])
+            for o in range(O):
+                for zl in range(ZL):
+                    first = (o * ZL + zl) * B_CHUNK
+                    z = (zq * ZL + zl) * HALVES
+                    nc.sync.dma_start(
+                        out=out[bq * B_CHUNK : (bq + 1) * B_CHUNK, z : z + HALVES, o].rearrange(
+                            "b z p u q -> b z (p u q)"
                         ),
-                        in_=results[bq][zh * B_CHUNK : (zh + 1) * B_CHUNK].rearrange("k h o n -> k (h o n)"),
+                        in_=result[first : first + B_CHUNK],
                     )
 
         for unit in range(LOADS_AHEAD):
@@ -197,7 +195,7 @@ def tile_mpolinear2_pa_t_kernel(tc, t_first, mid_core0, mid_core1, out):
                     out=core0_grouped[rows, g, h].rearrange("k (p s) t -> k p s t", p=O),
                     in_=core0_raw[rows, g:I:GROUPS, :].rearrange("k t (s p) -> k p s t", p=O),
                 )
-            nc.vector.tensor_copy(
+            nc.scalar.copy(
                 out=core1_grouped[rows, :, h],
                 in_=core1_raw[rows].rearrange("k (g t) n -> k g n t", t=PACK),
             )
@@ -212,24 +210,17 @@ def tile_mpolinear2_pa_t_kernel(tc, t_first, mid_core0, mid_core1, out):
             in_=core1_grouped[:].rearrange("k g h n t -> k (g h n t)"),
         )
 
-        def turn_over(unit, zh):
-            if unit < N_UNITS:
-                empty_bank(unit, zh)
-                transpose_bank(unit + 1, zh)
-
-        for zh in (0, 3, 1, 2):
-            transpose_bank(0, zh)
+        for g in range(GROUPS):
+            for zl in range(ZL):
+                transpose_bank(0, g, zl)
         for step in range(N_STEPS):
-            round_mid(step - ROUND_LAG, 0)
-            first_contraction(step - FIRST_LAG, 0)
-            turn_over(step, 0)
-            turn_over(step, 3)
-            turn_over(step, 1)
-            round_mid(step - ROUND_LAG, 1)
-            first_contraction(step - FIRST_LAG, 1)
+            quantise_mid(step - MID_LAG)
+            for half in range(2):
+                turn_over(step, half, 0)
+                turn_over(step, half, 1)
+                round_mid(step - ROUND_LAG, half)
+                quantise_unit(step - QUANTISE_LAG, half)
+                first_contraction(step - FIRST_LAG, half)
             second_contraction(step - SECOND_LAG)
-            turn_over(step, 2)
-            quantise_unit(step - QUANTISE_LAG)
-            quantise_mid(step - ROUND_LAG)
             finish(step - FINISH_LAG)
             load(step + LOADS_AHEAD)

@@ -39,7 +39,7 @@ def tile_mpolinear2_pa_t_kernel(tc, t_first, mid_core0, mid_core1, out):
     nc = tc.nc
     with ExitStack() as ctx:
         consts = ctx.enter_context(tc.tile_pool(name="consts", bufs=1))
-        raw_pool = ctx.enter_context(tc.tile_pool(name="raw_pool", bufs=LOADS_AHEAD))
+        raw_pool = ctx.enter_context(tc.tile_pool(name="raw_pool", bufs=LOADS_AHEAD * GROUPS))
         work = ctx.enter_context(tc.tile_pool(name="work", bufs=3))
         psum_t = ctx.enter_context(tc.psum_pool(name="psum_t", bufs=GROUPS * ZL))
         psum_1 = ctx.enter_context(tc.psum_pool(name="psum_1", bufs=HALVES))
@@ -56,22 +56,26 @@ def tile_mpolinear2_pa_t_kernel(tc, t_first, mid_core0, mid_core1, out):
             if unit >= N_UNITS:
                 return
             bq, yg, zq = split_unit(unit)
-            raw[unit] = raw_pool.tile([P, I, ZL * HALVES * R * O], BF16, name="raw")
-            for y in range(PACK):
-                nc.sync.dma_start(
-                    out=raw[unit][y:P:PACK],
-                    in_=t_first[
-                        bq * B_CHUNK : (bq + 1) * B_CHUNK, :, yg * PACK + y, zq * ZL * HALVES : (zq + 1) * ZL * HALVES
-                    ].rearrange("b x z r o -> b x (z r o)"),
-                )
+            for g in range(GROUPS):
+                raw[unit, g] = raw_pool.tile([P, PACK, ZL * HALVES * R * O], BF16, name="raw")
+                for y in range(PACK):
+                    nc.sync.dma_start(
+                        out=raw[unit, g][y:P:PACK],
+                        in_=t_first[
+                            bq * B_CHUNK : (bq + 1) * B_CHUNK,
+                            g:I:GROUPS,
+                            yg * PACK + y,
+                            zq * ZL * HALVES : (zq + 1) * ZL * HALVES,
+                        ].rearrange("b x z r o -> b x (z r o)"),
+                    )
 
         def transpose_bank(unit, g, zl):
             if unit >= N_UNITS:
                 return
             bank = psum_t.tile([P, PACK, P], F32, name="bank")
-            words = raw[unit][:].bitcast(F32)
+            words = raw[unit, g][:].bitcast(F32)
             for t in range(PACK):
-                nc.tensor.transpose(bank[:, t, :], words[:, g + GROUPS * t, zl * P : (zl + 1) * P], ident[:])
+                nc.tensor.transpose(bank[:, t, :], words[:, t, zl * P : (zl + 1) * P], ident[:])
             banks[unit, g, zl] = bank
 
         def turn_over(unit, g, zl):

@@ -22,15 +22,14 @@ B_CHUNK = P // PACK
 N_BQ = B // B_CHUNK
 N_UNITS = N_BQ * GROUPS * ZQ
 N_FINAL = N_BQ * ZQ * HALVES
-LOADS_AHEAD = 6
 
 QUANTISE_LAG = 1
-FIRST_LAG = 2
-ROUND_LAG = 3
-MID_LAG = 4
-SECOND_LAG = GROUPS * ZQ - ZQ + MID_LAG
+FIRST_LAG = 3
+ROUND_LAG = 4
+MID_LAG = 6
+SECOND_LAG = (GROUPS * ZQ - ZQ) * 2 + MID_LAG + 1
 FINISH_LAG = SECOND_LAG + 1
-N_STEPS = N_UNITS + FINISH_LAG
+N_STEPS = 2 * N_UNITS
 
 FLOPS = 2 * (B * I * I * O) * (I * R) * N_OUT + 2 * (B * I * O * O) * (I * R) * N_OUT
 
@@ -39,7 +38,7 @@ def tile_mpolinear2_pa_t_kernel(tc, t_first, mid_core0, mid_core1, out):
     nc = tc.nc
     with ExitStack() as ctx:
         consts = ctx.enter_context(tc.tile_pool(name="consts", bufs=1))
-        raw_pool = ctx.enter_context(tc.tile_pool(name="raw_pool", bufs=LOADS_AHEAD * GROUPS))
+        raw_pool = ctx.enter_context(tc.tile_pool(name="raw_pool", bufs=N_UNITS * GROUPS))
         work = ctx.enter_context(tc.tile_pool(name="work", bufs=3))
         psum_t = ctx.enter_context(tc.psum_pool(name="psum_t", bufs=GROUPS * ZL))
         psum_1 = ctx.enter_context(tc.psum_pool(name="psum_1", bufs=HALVES))
@@ -53,8 +52,6 @@ def tile_mpolinear2_pa_t_kernel(tc, t_first, mid_core0, mid_core1, out):
             return unit // (GROUPS * ZQ), unit // ZQ % GROUPS, unit % ZQ
 
         def load(unit):
-            if unit >= N_UNITS:
-                return
             bq, yg, zq = split_unit(unit)
             for g in range(GROUPS):
                 raw[unit, g] = raw_pool.tile([P, PACK, ZL * HALVES * R * O], BF16, name="raw")
@@ -102,31 +99,38 @@ def tile_mpolinear2_pa_t_kernel(tc, t_first, mid_core0, mid_core1, out):
                 in_=grouped[unit][:, g].rearrange("k o z c t -> k (o z c t)"),
             )
 
-        def first_contraction(unit, h):
-            if not 0 <= unit < N_UNITS:
-                return
-            acc = psum_1.tile([P, BANK], F32, name="acc")
-            for g in range(GROUPS):
-                nc.tensor.matmul_mx(
-                    out=acc[:],
-                    lhsT=core0_codes[:, g, h].bitcast(FP8X4),
-                    lhsT_scale=core0_scales[:, g, h],
-                    rhs=codes[unit][:, g].bitcast(FP8X4),
-                    rhs_scale=scales[unit][:, g],
-                    start=(g == 0),
-                    stop=(g == GROUPS - 1),
-                )
-            accs[unit, h] = acc
+        def first_pass(acc, unit, h, g):
+            nc.tensor.matmul_mx(
+                out=acc[:],
+                lhsT=core0_codes[:, g, h].bitcast(FP8X4),
+                lhsT_scale=core0_scales[:, g, h],
+                rhs=codes[unit][:, g].bitcast(FP8X4),
+                rhs_scale=scales[unit][:, g],
+                start=(g == 0),
+                stop=(g == GROUPS - 1),
+            )
 
-        def round_mid(unit, h):
-            if not 0 <= unit < N_UNITS:
+        def new_acc(unit, h):
+            if 2 * unit + h + FIRST_LAG >= N_STEPS - 1:
+                return psum_t.tile([P, BANK], F32, name="bank")
+            return psum_1.tile([P, BANK], F32, name="acc")
+
+        def first_contraction(unit, h):
+            if unit < 0:
+                return
+            accs[unit, h] = new_acc(unit, h)
+            for g in range(GROUPS):
+                first_pass(accs[unit, h], unit, h, g)
+
+        def round_mid(unit, h, copy):
+            if unit < 0:
                 return
             if h == 0:
                 mids[unit] = work.tile([P, HALVES, BANK], BF16, name="mid", align_bytes=64)
-            nc.scalar.copy(out=mids[unit][:, h], in_=accs[unit, h][:])
+            copy(out=mids[unit][:, h], in_=accs[unit, h][:])
 
         def quantise_mid(unit):
-            if not 0 <= unit < N_UNITS:
+            if unit < 0:
                 return
             bq, yg, zq = split_unit(unit)
             if yg == 0 and zq == 0:
@@ -138,93 +142,163 @@ def tile_mpolinear2_pa_t_kernel(tc, t_first, mid_core0, mid_core1, out):
                 in_=mids[unit][:].rearrange("k h n -> k (h n)"),
             )
 
+        def second_pass(acc2, bq, yg, zq, h):
+            nc.tensor.matmul_mx(
+                out=acc2,
+                lhsT=mid_codes[bq][:, yg, zq, h].bitcast(FP8X4),
+                lhsT_scale=mid_scales[bq][:, yg, zq, h],
+                rhs=core1_codes[:, yg].bitcast(FP8X4),
+                rhs_scale=core1_scales[:, yg],
+                start=(yg == 0),
+                stop=(yg == GROUPS - 1),
+            )
+
+        def split_group(group):
+            return group // (ZQ * HALVES), group // HALVES % ZQ, group % HALVES
+
         def second_contraction(group):
-            if not 0 <= group < N_FINAL:
+            if group < 0:
                 return
-            bq, zq, h = group // (ZQ * HALVES), group // HALVES % ZQ, group % HALVES
+            bq, zq, h = split_group(group)
             if h == 0:
                 accs2[bq, zq] = psum_2.tile([P, HALVES, HALVES * N_OUT], F32, name="acc2")
             for yg in range(GROUPS):
-                nc.tensor.matmul_mx(
-                    out=accs2[bq, zq][:, h],
-                    lhsT=mid_codes[bq][:, yg, zq, h].bitcast(FP8X4),
-                    lhsT_scale=mid_scales[bq][:, yg, zq, h],
-                    rhs=core1_codes[:, yg].bitcast(FP8X4),
-                    rhs_scale=core1_scales[:, yg],
-                    start=(yg == 0),
-                    stop=(yg == GROUPS - 1),
-                )
+                second_pass(accs2[bq, zq][:, h], bq, yg, zq, h)
 
-        def finish(group):
-            if not 0 <= group < N_FINAL or group % HALVES != HALVES - 1:
-                return
-            bq, zq = group // (ZQ * HALVES), group // HALVES % ZQ
-            result = work.tile([P, HALVES, HALVES * N_OUT], F32, name="result")
-            nc.scalar.copy(out=result[:], in_=accs2[bq, zq][:])
+        def store(result, bq, zq, h_first, n_h, queue):
             for o in range(O):
                 for zl in range(ZL):
                     first = (o * ZL + zl) * B_CHUNK
-                    z = (zq * ZL + zl) * HALVES
-                    nc.sync.dma_start(
-                        out=out[bq * B_CHUNK : (bq + 1) * B_CHUNK, z : z + HALVES, o].rearrange(
-                            "b z p u q -> b z (p u q)"
-                        ),
+                    z = (zq * ZL + zl) * HALVES + h_first
+                    queue.dma_start(
+                        out=out[bq * B_CHUNK : (bq + 1) * B_CHUNK, z : z + n_h, o].rearrange("b z p u q -> b z (p u q)"),
                         in_=result[first : first + B_CHUNK],
                     )
 
-        for unit in range(LOADS_AHEAD):
-            load(unit)
-
-        ident = consts.tile([P, P], F32, name="ident")
-        make_identity(nc, ident[:])
+        def finish(group):
+            if group < 0 or group % HALVES != HALVES - 1:
+                return
+            bq, zq = split_group(group)[:2]
+            result = work.tile([P, HALVES, HALVES * N_OUT], F32, name="result")
+            nc.scalar.copy(out=result[:], in_=accs2[bq, zq][:])
+            store(result, bq, zq, 0, HALVES, nc.sync)
 
         core0_raw = consts.tile([P, I, N_OUT], BF16, name="core0_raw")
         core1_raw = consts.tile([P, I, N_OUT], BF16, name="core1_raw")
-        for h in range(HALVES):
-            rows = slice(h * R, (h + 1) * R)
-            nc.scalar.dma_start(out=core0_raw[rows], in_=mid_core0.rearrange("x r s p -> r x (s p)"))
-            nc.scalar.dma_start(out=core1_raw[rows], in_=mid_core1.rearrange("y s u q -> s y (u q)"))
         core0_grouped = consts.tile([P, GROUPS, HALVES, N_OUT, PACK], BF16, name="core0_grouped", align_bytes=64)
         core1_grouped = consts.tile([P, GROUPS, HALVES, N_OUT, PACK], BF16, name="core1_grouped", align_bytes=64)
         core0_codes = consts.tile([P, GROUPS, HALVES, N_OUT], U32, name="core0_codes", align_bytes=64)
         core0_scales = consts.tile([P, GROUPS, HALVES, N_OUT], U8, name="core0_scales", align_bytes=64)
         core1_codes = consts.tile([P, GROUPS, HALVES * N_OUT], U32, name="core1_codes", align_bytes=64)
         core1_scales = consts.tile([P, GROUPS, HALVES * N_OUT], U8, name="core1_scales", align_bytes=64)
-        nc.vector.memset(core0_grouped[:], 0.0)
-        nc.vector.memset(core1_grouped[:], 0.0)
+
+        spark = consts.tile([P, 2], F32, name="spark")
+        nc.vector.memset(spark[:], 0.0)
+        nc.scalar.copy(out=spark[:, 1:2], in_=spark[:, 0:1])
+
+        ident = consts.tile([P, P], F32, name="ident")
+        make_identity(nc, ident[:])
+        nc.gpsimd.memset(core0_grouped[:].rearrange("k g h n t -> k (g h n t)").bitcast(F32), 0.0)
+        nc.gpsimd.memset(core1_grouped[:].rearrange("k g h n t -> k (g h n t)").bitcast(F32), 0.0)
+
+        for unit in range(N_UNITS):
+            load(unit)
+            for h in range(HALVES):
+                rows = slice(h * R, (h + 1) * R)
+                if unit == 0:
+                    nc.sync.dma_start(out=core0_raw[rows], in_=mid_core0.rearrange("x r s p -> r x (s p)"))
+                if unit == 1:
+                    nc.sync.dma_start(out=core1_raw[rows], in_=mid_core1.rearrange("y s u q -> s y (u q)"))
+
         for h in range(HALVES):
             rows = slice(h * R, (h + 1) * R)
             for g in range(GROUPS):
-                nc.vector.tensor_copy(
+                nc.gpsimd.tensor_scalar(
                     out=core0_grouped[rows, g, h].rearrange("k (p s) t -> k p s t", p=O),
-                    in_=core0_raw[rows, g:I:GROUPS, :].rearrange("k t (s p) -> k p s t", p=O),
+                    in0=core0_raw[rows, g:I:GROUPS, :].rearrange("k t (s p) -> k p s t", p=O),
+                    scalar1=1.0,
+                    scalar2=0.0,
+                    op0=mybir.AluOpType.mult,
+                    op1=mybir.AluOpType.add,
                 )
-            nc.scalar.copy(
+        for h in range(HALVES):
+            rows = slice(h * R, (h + 1) * R)
+            nc.gpsimd.tensor_scalar(
                 out=core1_grouped[rows, :, h],
-                in_=core1_raw[rows].rearrange("k (g t) n -> k g n t", t=PACK),
+                in0=core1_raw[rows].rearrange("k (g t) n -> k g n t", t=PACK),
+                scalar1=1.0,
+                scalar2=0.0,
+                op0=mybir.AluOpType.mult,
+                op1=mybir.AluOpType.add,
             )
-        nc.vector.quantize_mx(
-            out=core0_codes[:].rearrange("k g h m -> k (g h m)").bitcast(FP8X4),
-            scales=core0_scales[:].rearrange("k g h m -> k (g h m)"),
-            in_=core0_grouped[:].rearrange("k g h m t -> k (g h m t)"),
-        )
-        nc.vector.quantize_mx(
-            out=core1_codes[:].rearrange("k g n -> k (g n)").bitcast(FP8X4),
-            scales=core1_scales[:].rearrange("k g n -> k (g n)"),
-            in_=core1_grouped[:].rearrange("k g h n t -> k (g h n t)"),
-        )
+
+        def quantise_core0():
+            nc.vector.quantize_mx(
+                out=core0_codes[:].rearrange("k g h m -> k (g h m)").bitcast(FP8X4),
+                scales=core0_scales[:].rearrange("k g h m -> k (g h m)"),
+                in_=core0_grouped[:].rearrange("k g h m t -> k (g h m t)"),
+            )
+
+        def quantise_core1():
+            nc.vector.quantize_mx(
+                out=core1_codes[:].rearrange("k g n -> k (g n)").bitcast(FP8X4),
+                scales=core1_scales[:].rearrange("k g n -> k (g n)"),
+                in_=core1_grouped[:].rearrange("k g h n t -> k (g h n t)"),
+            )
 
         for g in range(GROUPS):
             for zl in range(ZL):
                 transpose_bank(0, g, zl)
         for step in range(N_STEPS):
-            quantise_mid(step - MID_LAG)
-            for half in range(2):
-                turn_over(step, half, 0)
-                turn_over(step, half, 1)
-                round_mid(step - ROUND_LAG, half)
-                quantise_unit(step - QUANTISE_LAG, half)
-                first_contraction(step - FIRST_LAG, half)
-            second_contraction(step - SECOND_LAG)
-            finish(step - FINISH_LAG)
-            load(step + LOADS_AHEAD)
+            turn_over(step // 2, step % 2, 0)
+            first_contraction((step - FIRST_LAG) // 2, (step - FIRST_LAG) % 2)
+            if (step - SECOND_LAG) % 2 == 0:
+                second_contraction((step - SECOND_LAG) // 2)
+            turn_over(step // 2, step % 2, 1)
+            round_mid((step - ROUND_LAG) // 2, (step - ROUND_LAG) % 2, nc.scalar.copy)
+            quantise_unit((step - QUANTISE_LAG) // 2, (step - QUANTISE_LAG) % 2)
+            if step == FIRST_LAG - 1:
+                quantise_core0()
+            if step == SECOND_LAG - 1:
+                quantise_core1()
+            if (step - MID_LAG) % 2 == 0:
+                quantise_mid((step - MID_LAG) // 2)
+            if (step - FINISH_LAG) % 2 == 0:
+                finish((step - FINISH_LAG) // 2)
+
+        last, before = N_UNITS - 1, N_UNITS - 2
+        bq, zq = N_BQ - 1, ZQ - 1
+        first_contraction(before, HALVES - 1)
+        for h in range(HALVES):
+            accs[last, h] = new_acc(last, h)
+            first_pass(accs[last, h], last, h, 0)
+        quantise_unit(last, 1)
+        for group in range((N_STEPS - 1 - SECOND_LAG) // 2 + 1, N_FINAL - 2 * HALVES):
+            second_contraction(group)
+        for h in range(HALVES):
+            first_pass(accs[last, h], last, h, 1)
+        for h in range(HALVES):
+            round_mid(before, h, nc.scalar.copy)
+        for group in range((N_STEPS - 1 - FINISH_LAG) // 2 + 1, N_FINAL - 2 * HALVES):
+            finish(group)
+        for unit in range((N_STEPS - 1 - MID_LAG) // 2 + 1, last):
+            quantise_mid(unit)
+        round_mid(last, 0, nc.scalar.copy)
+        round_mid(last, 1, nc.vector.tensor_copy)
+        for group in range(N_FINAL - 2 * HALVES, N_FINAL - HALVES):
+            second_contraction(group)
+        finish(N_FINAL - HALVES - 1)
+        halves = []
+        for h in range(HALVES):
+            halves.append(psum_t.tile([P, HALVES * N_OUT], F32, name="bank"))
+            second_pass(halves[h][:], bq, 0, zq, h)
+        quantise_mid(last)
+        for h in range(HALVES):
+            second_pass(halves[h][:], bq, 1, zq, h)
+        for h in range(HALVES):
+            result = work.tile([P, 1, HALVES * N_OUT], F32, name="last_result")
+            if h == 0:
+                nc.scalar.copy(out=result[:, 0], in_=halves[h][:])
+            else:
+                nc.vector.tensor_copy(out=result[:, 0], in_=halves[h][:])
+            store(result, bq, zq, h, 1, nc.scalar if h == 0 else nc.sync)

@@ -29,6 +29,7 @@ ROUND_LAG = 4
 MID_LAG = 6
 SECOND_LAG = (GROUPS * ZQ - ZQ) * 2 + MID_LAG + 1
 FINISH_LAG = SECOND_LAG + 1
+SEPARATE_AHEAD = 3
 N_STEPS = 2 * N_UNITS
 
 FLOPS = 2 * (B * I * I * O) * (I * R) * N_OUT + 2 * (B * I * O * O) * (I * R) * N_OUT
@@ -66,13 +67,38 @@ def tile_mpolinear2_pa_t_kernel(tc, t_first, mid_core0, mid_core1, out):
                         ].rearrange("b x z r o -> b x (z r o)"),
                     )
 
+        def is_separated(unit, g, zl):
+            return unit >= SEPARATE_AHEAD and g == GROUPS - 1 and zl == ZL - 1
+
+        def separate(unit, u):
+            if not SEPARATE_AHEAD <= unit < N_UNITS:
+                return
+            nc.gpsimd.tensor_scalar(
+                out=separated(unit, u).rearrange("k (o n e) -> k o n e", o=O, e=2),
+                in0=raw[unit, GROUPS - 1][:, 2 * u : 2 * u + 2, (ZL - 1) * 2 * P :].rearrange("k e (n o) -> k o n e", o=O),
+                scalar1=1.0,
+                scalar2=0.0,
+                op0=mybir.AluOpType.mult,
+                op1=mybir.AluOpType.add,
+            )
+
+        def separated(unit, u):
+            older = grouped[unit - SEPARATE_AHEAD][:, u].rearrange("k o z c t -> k (o z c t)")
+            return older[:, : O * P * 2]
+
         def transpose_bank(unit, g, zl):
             if unit >= N_UNITS:
                 return
             bank = psum_t.tile([P, PACK, P], F32, name="bank")
-            words = raw[unit, g][:].bitcast(F32)
-            for t in range(PACK):
-                nc.tensor.transpose(bank[:, t, :], words[:, t, zl * P : (zl + 1) * P], ident[:])
+            if is_separated(unit, g, zl):
+                for u in range(2):
+                    words = separated(unit, u).bitcast(F32)
+                    for o in range(O):
+                        nc.tensor.transpose(bank[:, 2 * o + u, :], words[:, o * P : (o + 1) * P], ident[:])
+            else:
+                words = raw[unit, g][:].bitcast(F32)
+                for t in range(PACK):
+                    nc.tensor.transpose(bank[:, t, :], words[:, t, zl * P : (zl + 1) * P], ident[:])
             banks[unit, g, zl] = bank
 
         def turn_over(unit, g, zl):
@@ -81,7 +107,13 @@ def tile_mpolinear2_pa_t_kernel(tc, t_first, mid_core0, mid_core1, out):
             if g == 0 and zl == 0:
                 grouped[unit] = work.tile([P, GROUPS, O, ZL, P, PACK], BF16, name="grouped", align_bytes=64)
             halves = banks[unit, g, zl][:].bitcast(BF16).rearrange("k t (c o) -> k o c t", o=O)
-            if zl == 0:
+            if is_separated(unit, g, zl):
+                words = grouped[unit][:].rearrange("k g o z c t -> k (g o z c t)").bitcast(F32)
+                words = words.rearrange("k (g o z c u) -> k g o z c u", g=GROUPS, o=O, z=ZL, u=2)
+                nc.vector.tensor_copy(
+                    out=words[:, g, :, zl], in_=banks[unit, g, zl][:].rearrange("k (o u) c -> k o c u", o=O)
+                )
+            elif zl == 0:
                 nc.scalar.copy(out=grouped[unit][:, g, :, zl], in_=halves)
             else:
                 nc.vector.tensor_copy(out=grouped[unit][:, g, :, zl], in_=halves)
@@ -180,7 +212,8 @@ def tile_mpolinear2_pa_t_kernel(tc, t_first, mid_core0, mid_core1, out):
                 return
             bq, zq = split_group(group)[:2]
             result = work.tile([P, HALVES, HALVES * N_OUT], F32, name="result")
-            nc.scalar.copy(out=result[:], in_=accs2[bq, zq][:])
+            copy = nc.scalar.copy if zq == 0 else nc.vector.tensor_copy
+            copy(out=result[:], in_=accs2[bq, zq][:])
             store(result, bq, zq, 0, HALVES, nc.sync)
 
         core0_raw = consts.tile([P, I, N_OUT], BF16, name="core0_raw")
@@ -221,7 +254,8 @@ def tile_mpolinear2_pa_t_kernel(tc, t_first, mid_core0, mid_core1, out):
                     op0=mybir.AluOpType.mult,
                     op1=mybir.AluOpType.add,
                 )
-        for h in range(HALVES):
+
+        def lay_out_core1(h):
             rows = slice(h * R, (h + 1) * R)
             nc.gpsimd.tensor_scalar(
                 out=core1_grouped[rows, :, h],
@@ -257,6 +291,9 @@ def tile_mpolinear2_pa_t_kernel(tc, t_first, mid_core0, mid_core1, out):
             turn_over(step // 2, step % 2, 1)
             round_mid((step - ROUND_LAG) // 2, (step - ROUND_LAG) % 2, nc.scalar.copy)
             quantise_unit((step - QUANTISE_LAG) // 2, (step - QUANTISE_LAG) % 2)
+            separate((step - QUANTISE_LAG) // 2 + SEPARATE_AHEAD, (step - QUANTISE_LAG) % 2)
+            if step in (3, 4):
+                lay_out_core1(step - 3)
             if step == FIRST_LAG - 1:
                 quantise_core0()
             if step == SECOND_LAG - 1:

@@ -41,6 +41,7 @@ def tile_mpolinear2_pa_t_kernel(tc, t_first, mid_core0, mid_core1, out):
         consts = ctx.enter_context(tc.tile_pool(name="consts", bufs=1))
         raw_pool = ctx.enter_context(tc.tile_pool(name="raw_pool", bufs=N_UNITS * GROUPS))
         work = ctx.enter_context(tc.tile_pool(name="work", bufs=3))
+        grouped_pool = ctx.enter_context(tc.tile_pool(name="grouped_pool", bufs=SEPARATE_AHEAD + 1))
         psum_t = ctx.enter_context(tc.psum_pool(name="psum_t", bufs=GROUPS * ZL))
         psum_1 = ctx.enter_context(tc.psum_pool(name="psum_1", bufs=HALVES))
         psum_2 = ctx.enter_context(tc.psum_pool(name="psum_2", bufs=2))
@@ -105,7 +106,7 @@ def tile_mpolinear2_pa_t_kernel(tc, t_first, mid_core0, mid_core1, out):
             if unit >= N_UNITS:
                 return
             if g == 0 and zl == 0:
-                grouped[unit] = work.tile([P, GROUPS, O, ZL, P, PACK], BF16, name="grouped", align_bytes=64)
+                grouped[unit] = grouped_pool.tile([P, GROUPS, O, ZL, P, PACK], BF16, name="grouped", align_bytes=64)
             halves = banks[unit, g, zl][:].bitcast(BF16).rearrange("k t (c o) -> k o c t", o=O)
             if is_separated(unit, g, zl):
                 words = grouped[unit][:].rearrange("k g o z c t -> k (g o z c t)").bitcast(F32)

@@ -24,13 +24,12 @@ N_UNITS = N_BQ * GROUPS * ZQ
 N_FINAL = N_BQ * ZQ * HALVES
 
 QUANTISE_LAG = 1
-FIRST_LAG = 3
-ROUND_LAG = 4
-MID_LAG = 6
-SECOND_LAG = (GROUPS * ZQ - ZQ) * 2 + MID_LAG + 1
-FINISH_LAG = SECOND_LAG + 1
+FIRST_LAG = 1
+ROUND_LAG = 2
+MID_LAG = 3
 SEPARATE_AHEAD = 3
-N_STEPS = 2 * N_UNITS
+SECOND_LAG = GROUPS * ZQ - ZQ + MID_LAG + 1
+FINISH_LAG = SECOND_LAG + 1
 
 FLOPS = 2 * (B * I * I * O) * (I * R) * N_OUT + 2 * (B * I * O * O) * (I * R) * N_OUT
 
@@ -41,7 +40,7 @@ def tile_mpolinear2_pa_t_kernel(tc, t_first, mid_core0, mid_core1, out):
         consts = ctx.enter_context(tc.tile_pool(name="consts", bufs=1))
         raw_pool = ctx.enter_context(tc.tile_pool(name="raw_pool", bufs=N_UNITS * GROUPS))
         work = ctx.enter_context(tc.tile_pool(name="work", bufs=3))
-        grouped_pool = ctx.enter_context(tc.tile_pool(name="grouped_pool", bufs=SEPARATE_AHEAD + 1))
+        mid_pool = ctx.enter_context(tc.tile_pool(name="mid_pool", bufs=4))
         psum_t = ctx.enter_context(tc.psum_pool(name="psum_t", bufs=GROUPS * ZL))
         psum_1 = ctx.enter_context(tc.psum_pool(name="psum_1", bufs=HALVES))
         psum_2 = ctx.enter_context(tc.psum_pool(name="psum_2", bufs=2))
@@ -69,10 +68,10 @@ def tile_mpolinear2_pa_t_kernel(tc, t_first, mid_core0, mid_core1, out):
                     )
 
         def is_separated(unit, g, zl):
-            return unit >= SEPARATE_AHEAD and g == GROUPS - 1 and zl == ZL - 1
+            return unit >= MID_LAG + SEPARATE_AHEAD and g == GROUPS - 1 and zl == ZL - 1
 
         def separate(unit, u):
-            if not SEPARATE_AHEAD <= unit < N_UNITS:
+            if not MID_LAG + SEPARATE_AHEAD <= unit < N_UNITS:
                 return
             nc.gpsimd.tensor_scalar(
                 out=separated(unit, u).rearrange("k (o n e) -> k o n e", o=O, e=2),
@@ -84,8 +83,7 @@ def tile_mpolinear2_pa_t_kernel(tc, t_first, mid_core0, mid_core1, out):
             )
 
         def separated(unit, u):
-            older = grouped[unit - SEPARATE_AHEAD][:, u].rearrange("k o z c t -> k (o z c t)")
-            return older[:, : O * P * 2]
+            return mids[unit - SEPARATE_AHEAD - MID_LAG][:, u]
 
         def transpose_bank(unit, g, zl):
             if unit >= N_UNITS:
@@ -105,8 +103,8 @@ def tile_mpolinear2_pa_t_kernel(tc, t_first, mid_core0, mid_core1, out):
         def turn_over(unit, g, zl):
             if unit >= N_UNITS:
                 return
-            if g == 0 and zl == 0:
-                grouped[unit] = grouped_pool.tile([P, GROUPS, O, ZL, P, PACK], BF16, name="grouped", align_bytes=64)
+            if unit not in grouped:
+                grouped[unit] = work.tile([P, GROUPS, O, ZL, P, PACK], BF16, name="grouped", align_bytes=64)
             halves = banks[unit, g, zl][:].bitcast(BF16).rearrange("k t (c o) -> k o c t", o=O)
             if is_separated(unit, g, zl):
                 words = grouped[unit][:].rearrange("k g o z c t -> k (g o z c t)").bitcast(F32)
@@ -120,16 +118,16 @@ def tile_mpolinear2_pa_t_kernel(tc, t_first, mid_core0, mid_core1, out):
                 nc.vector.tensor_copy(out=grouped[unit][:, g, :, zl], in_=halves)
             transpose_bank(unit + 1, g, zl)
 
-        def quantise_unit(unit, g):
+        def quantise_unit(unit, g, n_g):
             if not 0 <= unit < N_UNITS:
                 return
             if g == 0:
                 codes[unit] = work.tile([P, GROUPS, BANK], U32, name="codes", align_bytes=64)
                 scales[unit] = work.tile([P, GROUPS, BANK], U8, name="scales", align_bytes=64)
             nc.vector.quantize_mx(
-                out=codes[unit][:, g].bitcast(FP8X4),
-                scales=scales[unit][:, g],
-                in_=grouped[unit][:, g].rearrange("k o z c t -> k (o z c t)"),
+                out=codes[unit][:, g : g + n_g].rearrange("k g n -> k (g n)").bitcast(FP8X4),
+                scales=scales[unit][:, g : g + n_g].rearrange("k g n -> k (g n)"),
+                in_=grouped[unit][:, g : g + n_g].rearrange("k g o z c t -> k (g o z c t)"),
             )
 
         def first_pass(acc, unit, h, g):
@@ -144,7 +142,7 @@ def tile_mpolinear2_pa_t_kernel(tc, t_first, mid_core0, mid_core1, out):
             )
 
         def new_acc(unit, h):
-            if 2 * unit + h + FIRST_LAG >= N_STEPS - 1:
+            if unit >= N_UNITS - 1 - FIRST_LAG:
                 return psum_t.tile([P, BANK], F32, name="bank")
             return psum_1.tile([P, BANK], F32, name="acc")
 
@@ -159,7 +157,7 @@ def tile_mpolinear2_pa_t_kernel(tc, t_first, mid_core0, mid_core1, out):
             if unit < 0:
                 return
             if h == 0:
-                mids[unit] = work.tile([P, HALVES, BANK], BF16, name="mid", align_bytes=64)
+                mids[unit] = mid_pool.tile([P, HALVES, BANK], BF16, name="mid", align_bytes=64)
             copy(out=mids[unit][:, h], in_=accs[unit, h][:])
 
         def quantise_mid(unit):
@@ -282,44 +280,47 @@ def tile_mpolinear2_pa_t_kernel(tc, t_first, mid_core0, mid_core1, out):
             )
 
         for g in range(GROUPS):
-            for zl in range(ZL):
+            for zl in (0, 1) if g == 0 else (1, 0):
                 transpose_bank(0, g, zl)
-        for step in range(N_STEPS):
-            turn_over(step // 2, step % 2, 0)
-            first_contraction((step - FIRST_LAG) // 2, (step - FIRST_LAG) % 2)
-            if (step - SECOND_LAG) % 2 == 0:
-                second_contraction((step - SECOND_LAG) // 2)
-            turn_over(step // 2, step % 2, 1)
-            round_mid((step - ROUND_LAG) // 2, (step - ROUND_LAG) % 2, nc.scalar.copy)
-            quantise_unit((step - QUANTISE_LAG) // 2, (step - QUANTISE_LAG) % 2)
-            separate((step - QUANTISE_LAG) // 2 + SEPARATE_AHEAD, (step - QUANTISE_LAG) % 2)
-            if step in (3, 4):
-                lay_out_core1(step - 3)
-            if step == FIRST_LAG - 1:
+        for step in range(N_UNITS):
+            turn_over(step, 0, 0)
+            turn_over(step, 0, 1)
+            round_mid(step - ROUND_LAG, 0, nc.scalar.copy)
+            first_contraction(step - FIRST_LAG - 1, 1)
+            turn_over(step, 1, 1)
+            turn_over(step, 1, 0)
+            round_mid(step - ROUND_LAG, 1, nc.scalar.copy)
+            quantise_unit(step - QUANTISE_LAG, 0, GROUPS)
+            if step == FIRST_LAG:
                 quantise_core0()
             if step == SECOND_LAG - 1:
                 quantise_core1()
-            if (step - MID_LAG) % 2 == 0:
-                quantise_mid((step - MID_LAG) // 2)
-            if (step - FINISH_LAG) % 2 == 0:
-                finish((step - FINISH_LAG) // 2)
+            quantise_mid(step - MID_LAG)
+            separate(step + SEPARATE_AHEAD, 0)
+            separate(step + SEPARATE_AHEAD, 1)
+            if step in (2, 3):
+                lay_out_core1(step - 2)
+            first_contraction(step - FIRST_LAG, 0)
+            second_contraction(step - SECOND_LAG)
+            finish(step - FINISH_LAG)
 
         last, before = N_UNITS - 1, N_UNITS - 2
         bq, zq = N_BQ - 1, ZQ - 1
-        first_contraction(before, HALVES - 1)
+        first_contraction(before, 1)
+        quantise_unit(last, 0, 1)
+        quantise_unit(last, 1, 1)
+        for group in range(last - SECOND_LAG + 1, N_FINAL - 2 * HALVES):
+            second_contraction(group)
         for h in range(HALVES):
             accs[last, h] = new_acc(last, h)
             first_pass(accs[last, h], last, h, 0)
-        quantise_unit(last, 1)
-        for group in range((N_STEPS - 1 - SECOND_LAG) // 2 + 1, N_FINAL - 2 * HALVES):
-            second_contraction(group)
         for h in range(HALVES):
             first_pass(accs[last, h], last, h, 1)
         for h in range(HALVES):
             round_mid(before, h, nc.scalar.copy)
-        for group in range((N_STEPS - 1 - FINISH_LAG) // 2 + 1, N_FINAL - 2 * HALVES):
+        for group in range(last - FINISH_LAG + 1, N_FINAL - 2 * HALVES):
             finish(group)
-        for unit in range((N_STEPS - 1 - MID_LAG) // 2 + 1, last):
+        for unit in range(last - MID_LAG + 1, last):
             quantise_mid(unit)
         round_mid(last, 0, nc.scalar.copy)
         round_mid(last, 1, nc.vector.tensor_copy)

@@ -15,6 +15,7 @@ B, I, R, O = 128, 8, 64, 2
 HALVES = P // R
 GROUPS = I // PACK
 N_OUT = R * O
+UNIT_RUN = 4 * R * O
 BANK = 512
 
 ZQ, ZL = 2, 2
@@ -38,7 +39,7 @@ def tile_mpolinear2_pa_t_kernel(tc, t_first, mid_core0, mid_core1, out):
     nc = tc.nc
     with ExitStack() as ctx:
         consts = ctx.enter_context(tc.tile_pool(name="consts", bufs=1))
-        raw_pool = ctx.enter_context(tc.tile_pool(name="raw_pool", bufs=N_UNITS * GROUPS))
+        raw_pool = ctx.enter_context(tc.tile_pool(name="raw_pool", bufs=N_UNITS // ZQ * GROUPS))
         work = ctx.enter_context(tc.tile_pool(name="work", bufs=3))
         mid_pool = ctx.enter_context(tc.tile_pool(name="mid_pool", bufs=4))
         psum_t = ctx.enter_context(tc.psum_pool(name="psum_t", bufs=GROUPS * ZL))
@@ -46,7 +47,7 @@ def tile_mpolinear2_pa_t_kernel(tc, t_first, mid_core0, mid_core1, out):
         psum_2 = ctx.enter_context(tc.psum_pool(name="psum_2", bufs=2))
         ctx.enter_context(tc.manual_schedule())
 
-        raw, banks, grouped, codes, scales = {}, {}, {}, {}, {}
+        pairs, raw, banks, grouped, codes, scales = {}, {}, {}, {}, {}, {}
         accs, mids, mid_codes, mid_scales, accs2 = {}, {}, {}, {}, {}
 
         def split_unit(unit):
@@ -55,15 +56,23 @@ def tile_mpolinear2_pa_t_kernel(tc, t_first, mid_core0, mid_core1, out):
         def load(unit):
             bq, yg, zq = split_unit(unit)
             for g in range(GROUPS):
-                raw[unit, g] = raw_pool.tile([P, PACK, ZL * HALVES * R * O], BF16, name="raw")
+                if zq == 0:
+                    pairs[bq, yg, g] = raw_pool.tile([P, PACK, ZQ, UNIT_RUN], BF16, name="raw")
+                raw[unit, g] = pairs[bq, yg, g][:, :, zq]
+                if unit == 0 or unit == 1:
+                    zqs = slice(zq, zq + 1)
+                elif zq == 0:
+                    zqs = slice(0, ZQ)
+                else:
+                    continue
                 for y in range(PACK):
                     nc.sync.dma_start(
-                        out=raw[unit, g][y:P:PACK],
+                        out=pairs[bq, yg, g][y:P:PACK, :, zqs].rearrange("k x q n -> k x (q n)"),
                         in_=t_first[
                             bq * B_CHUNK : (bq + 1) * B_CHUNK,
                             g:I:GROUPS,
                             yg * PACK + y,
-                            zq * ZL * HALVES : (zq + 1) * ZL * HALVES,
+                            zqs.start * ZL * HALVES : zqs.stop * ZL * HALVES,
                         ].rearrange("b x z r o -> b x (z r o)"),
                     )
 
@@ -95,7 +104,7 @@ def tile_mpolinear2_pa_t_kernel(tc, t_first, mid_core0, mid_core1, out):
                     for o in range(O):
                         nc.tensor.transpose(bank[:, 2 * o + u, :], words[:, o * P : (o + 1) * P], ident[:])
             else:
-                words = raw[unit, g][:].bitcast(F32)
+                words = raw[unit, g].bitcast(F32)
                 for t in range(PACK):
                     nc.tensor.transpose(bank[:, t, :], words[:, t, zl * P : (zl + 1) * P], ident[:])
             banks[unit, g, zl] = bank

@@ -10,6 +10,20 @@ U8 = mybir.dt.uint8
 FP8X4 = mybir.dt.float8_e4m3fn_x4
 
 P = 128
+S_EXTRA = ()
+SEP = (5, 7, 9, 11, 13, 15)
+FV = ()
+RV = ()
+GB = 3
+C0AT = 0
+C1AT = 2
+PREP = ((-1, 'G'), (-1, 'G'), (-1, 'G'), (-1, 'G'))
+TG = 0
+GS = 1
+LMODE = 1
+SPLIT0 = 0
+Q0AT = 1
+BANKACC = 28
 PACK = 4
 B, I, R, O = 128, 8, 64, 2
 HALVES = P // R
@@ -21,16 +35,17 @@ BANK = 512
 ZQ, ZL = 2, 2
 B_CHUNK = P // PACK
 N_BQ = B // B_CHUNK
+N_HEAD = 6
 N_UNITS = N_BQ * GROUPS * ZQ
 N_FINAL = N_BQ * ZQ * HALVES
 
-QUANTISE_LAG = 1
-FIRST_LAG = 1
-ROUND_LAG = 2
-MID_LAG = 3
-SEPARATE_AHEAD = 3
-SECOND_LAG = GROUPS * ZQ - ZQ + MID_LAG + 1
-FINISH_LAG = SECOND_LAG + 1
+L0 = 4
+RL = 1
+FL = 1
+Q1AT = 9
+L1 = ((4, 'G'), (4, 'G'), (4, 'G'), (4, 'G'))
+SEPARATE_AHEAD = 2
+N_STEPS = 2 * N_UNITS
 
 FLOPS = 2 * (B * I * I * O) * (I * R) * N_OUT + 2 * (B * I * O * O) * (I * R) * N_OUT
 
@@ -39,15 +54,17 @@ def tile_mpolinear2_pa_t_kernel(tc, t_first, mid_core0, mid_core1, out):
     nc = tc.nc
     with ExitStack() as ctx:
         consts = ctx.enter_context(tc.tile_pool(name="consts", bufs=1))
-        raw_pool = ctx.enter_context(tc.tile_pool(name="raw_pool", bufs=N_UNITS // ZQ * GROUPS))
+        raw_pool = ctx.enter_context(tc.tile_pool(name="raw_pool", bufs=(N_UNITS - N_HEAD) // ZQ * GROUPS))
+        head_pool = ctx.enter_context(tc.tile_pool(name="head_pool", bufs=N_HEAD * GROUPS))
         work = ctx.enter_context(tc.tile_pool(name="work", bufs=3))
-        mid_pool = ctx.enter_context(tc.tile_pool(name="mid_pool", bufs=4))
+        grouped_pool = ctx.enter_context(tc.tile_pool(name="grouped_pool", bufs=GB))
         psum_t = ctx.enter_context(tc.psum_pool(name="psum_t", bufs=GROUPS * ZL))
         psum_1 = ctx.enter_context(tc.psum_pool(name="psum_1", bufs=HALVES))
         psum_2 = ctx.enter_context(tc.psum_pool(name="psum_2", bufs=2))
         ctx.enter_context(tc.manual_schedule())
 
-        pairs, raw, banks, grouped, codes, scales = {}, {}, {}, {}, {}, {}
+        first_parts = {}
+        raw, banks, grouped, codes, scales = {}, {}, {}, {}, {}
         accs, mids, mid_codes, mid_scales, accs2 = {}, {}, {}, {}, {}
 
         def split_unit(unit):
@@ -56,18 +73,34 @@ def tile_mpolinear2_pa_t_kernel(tc, t_first, mid_core0, mid_core1, out):
         def load(unit):
             bq, yg, zq = split_unit(unit)
             for g in range(GROUPS):
-                if zq == 0:
-                    pairs[bq, yg, g] = raw_pool.tile([P, PACK, ZQ, UNIT_RUN], BF16, name="raw")
-                raw[unit, g] = pairs[bq, yg, g][:, :, zq]
-                if unit == 0 or unit == 1:
+                if unit == 0 and g < SPLIT0:
+                    parts = []
+                    for zl in range(ZL):
+                        tile = head_pool.tile([P, PACK, HALVES * R * O], BF16, name="first_raw")
+                        parts.append(tile)
+                        for y in range(PACK):
+                            nc.sync.dma_start(
+                                out=tile[y:P:PACK],
+                                in_=t_first[
+                                    bq * B_CHUNK : (bq + 1) * B_CHUNK, g:I:GROUPS, yg * PACK + y, zl * HALVES : (zl + 1) * HALVES
+                                ].rearrange("b x z r o -> b x (z r o)"),
+                            )
+                    first_parts[g] = parts
+                    continue
+                elif unit < N_HEAD:
                     zqs = slice(zq, zq + 1)
+                    tile = head_pool.tile([P, PACK, 1, UNIT_RUN], BF16, name="head_raw")
+                    raw[unit, g] = tile[:, :, 0]
                 elif zq == 0:
                     zqs = slice(0, ZQ)
+                    tile = raw_pool.tile([P, PACK, ZQ, UNIT_RUN], BF16, name="raw")
+                    for q in range(ZQ):
+                        raw[unit + q, g] = tile[:, :, q]
                 else:
                     continue
                 for y in range(PACK):
                     nc.sync.dma_start(
-                        out=pairs[bq, yg, g][y:P:PACK, :, zqs].rearrange("k x q n -> k x (q n)"),
+                        out=tile[y:P:PACK].rearrange("k x q n -> k x (q n)"),
                         in_=t_first[
                             bq * B_CHUNK : (bq + 1) * B_CHUNK,
                             g:I:GROUPS,
@@ -77,10 +110,10 @@ def tile_mpolinear2_pa_t_kernel(tc, t_first, mid_core0, mid_core1, out):
                     )
 
         def is_separated(unit, g, zl):
-            return unit >= MID_LAG + SEPARATE_AHEAD and g == GROUPS - 1 and zl == ZL - 1
+            return unit in SEP and g == GROUPS - 1 and zl == ZL - 1
 
         def separate(unit, u):
-            if not MID_LAG + SEPARATE_AHEAD <= unit < N_UNITS:
+            if unit >= N_UNITS or unit not in SEP:
                 return
             nc.gpsimd.tensor_scalar(
                 out=separated(unit, u).rearrange("k (o n e) -> k o n e", o=O, e=2),
@@ -92,7 +125,8 @@ def tile_mpolinear2_pa_t_kernel(tc, t_first, mid_core0, mid_core1, out):
             )
 
         def separated(unit, u):
-            return mids[unit - SEPARATE_AHEAD - MID_LAG][:, u]
+            older = grouped[unit - SEPARATE_AHEAD][:, u].rearrange("k o z c t -> k (o z c t)")
+            return older[:, : O * P * 2]
 
         def transpose_bank(unit, g, zl):
             if unit >= N_UNITS:
@@ -104,16 +138,19 @@ def tile_mpolinear2_pa_t_kernel(tc, t_first, mid_core0, mid_core1, out):
                     for o in range(O):
                         nc.tensor.transpose(bank[:, 2 * o + u, :], words[:, o * P : (o + 1) * P], ident[:])
             else:
-                words = raw[unit, g].bitcast(F32)
+                if unit == 0 and g in first_parts:
+                    words = first_parts[g][zl][:].bitcast(F32)
+                else:
+                    words = raw[unit, g].bitcast(F32)[:, :, zl * P : (zl + 1) * P]
                 for t in range(PACK):
-                    nc.tensor.transpose(bank[:, t, :], words[:, t, zl * P : (zl + 1) * P], ident[:])
+                    nc.tensor.transpose(bank[:, t, :], words[:, t], ident[:])
             banks[unit, g, zl] = bank
 
         def turn_over(unit, g, zl):
             if unit >= N_UNITS:
                 return
-            if unit not in grouped:
-                grouped[unit] = work.tile([P, GROUPS, O, ZL, P, PACK], BF16, name="grouped", align_bytes=64)
+            if g == 0 and zl == 0:
+                grouped[unit] = grouped_pool.tile([P, GROUPS, O, ZL, P, PACK], BF16, name="grouped", align_bytes=64)
             halves = banks[unit, g, zl][:].bitcast(BF16).rearrange("k t (c o) -> k o c t", o=O)
             if is_separated(unit, g, zl):
                 words = grouped[unit][:].rearrange("k g o z c t -> k (g o z c t)").bitcast(F32)
@@ -121,22 +158,22 @@ def tile_mpolinear2_pa_t_kernel(tc, t_first, mid_core0, mid_core1, out):
                 nc.vector.tensor_copy(
                     out=words[:, g, :, zl], in_=banks[unit, g, zl][:].rearrange("k (o u) c -> k o c u", o=O)
                 )
-            elif zl == 0:
+            elif zl == 0 or (unit, g) in S_EXTRA:
                 nc.scalar.copy(out=grouped[unit][:, g, :, zl], in_=halves)
             else:
                 nc.vector.tensor_copy(out=grouped[unit][:, g, :, zl], in_=halves)
             transpose_bank(unit + 1, g, zl)
 
-        def quantise_unit(unit, g, n_g):
+        def quantise_unit(unit, g):
             if not 0 <= unit < N_UNITS:
                 return
             if g == 0:
                 codes[unit] = work.tile([P, GROUPS, BANK], U32, name="codes", align_bytes=64)
                 scales[unit] = work.tile([P, GROUPS, BANK], U8, name="scales", align_bytes=64)
             nc.vector.quantize_mx(
-                out=codes[unit][:, g : g + n_g].rearrange("k g n -> k (g n)").bitcast(FP8X4),
-                scales=scales[unit][:, g : g + n_g].rearrange("k g n -> k (g n)"),
-                in_=grouped[unit][:, g : g + n_g].rearrange("k g o z c t -> k (g o z c t)"),
+                out=codes[unit][:, g].bitcast(FP8X4),
+                scales=scales[unit][:, g],
+                in_=grouped[unit][:, g].rearrange("k o z c t -> k (o z c t)"),
             )
 
         def first_pass(acc, unit, h, g):
@@ -151,7 +188,7 @@ def tile_mpolinear2_pa_t_kernel(tc, t_first, mid_core0, mid_core1, out):
             )
 
         def new_acc(unit, h):
-            if unit >= N_UNITS - 1 - FIRST_LAG:
+            if 2 * unit + h >= BANKACC:
                 return psum_t.tile([P, BANK], F32, name="bank")
             return psum_1.tile([P, BANK], F32, name="acc")
 
@@ -166,8 +203,8 @@ def tile_mpolinear2_pa_t_kernel(tc, t_first, mid_core0, mid_core1, out):
             if unit < 0:
                 return
             if h == 0:
-                mids[unit] = mid_pool.tile([P, HALVES, BANK], BF16, name="mid", align_bytes=64)
-            copy(out=mids[unit][:, h], in_=accs[unit, h][:])
+                mids[unit] = work.tile([P, HALVES, BANK], BF16, name="mid", align_bytes=64)
+            (nc.vector.tensor_copy if (unit, h) in RV else copy)(out=mids[unit][:, h], in_=accs[unit, h][:])
 
         def quantise_mid(unit):
             if unit < 0:
@@ -220,7 +257,7 @@ def tile_mpolinear2_pa_t_kernel(tc, t_first, mid_core0, mid_core1, out):
                 return
             bq, zq = split_group(group)[:2]
             result = work.tile([P, HALVES, HALVES * N_OUT], F32, name="result")
-            copy = nc.scalar.copy if zq == 0 else nc.vector.tensor_copy
+            copy = nc.vector.tensor_copy if (bq, zq) in FV else nc.scalar.copy
             copy(out=result[:], in_=accs2[bq, zq][:])
             store(result, bq, zq, 0, HALVES, nc.sync)
 
@@ -242,37 +279,48 @@ def tile_mpolinear2_pa_t_kernel(tc, t_first, mid_core0, mid_core1, out):
         nc.gpsimd.memset(core0_grouped[:].rearrange("k g h n t -> k (g h n t)").bitcast(F32), 0.0)
         nc.gpsimd.memset(core1_grouped[:].rearrange("k g h n t -> k (g h n t)").bitcast(F32), 0.0)
 
+        def load_core(raw_core, core):
+            for h in range(HALVES):
+                nc.sync.dma_start(out=raw_core[h * R : (h + 1) * R], in_=core)
+
         for unit in range(N_UNITS):
             load(unit)
-            for h in range(HALVES):
-                rows = slice(h * R, (h + 1) * R)
-                if unit == 0:
-                    nc.sync.dma_start(out=core0_raw[rows], in_=mid_core0.rearrange("x r s p -> r x (s p)"))
-                if unit == 1:
-                    nc.sync.dma_start(out=core1_raw[rows], in_=mid_core1.rearrange("y s u q -> s y (u q)"))
+            if unit == C0AT:
+                load_core(core0_raw, mid_core0.rearrange("x r s p -> r x (s p)"))
+            if unit == C1AT:
+                load_core(core1_raw, mid_core1.rearrange("y s u q -> s y (u q)"))
 
-        for h in range(HALVES):
+        def lay_out_core0(h, g, how):
             rows = slice(h * R, (h + 1) * R)
-            for g in range(GROUPS):
-                nc.gpsimd.tensor_scalar(
-                    out=core0_grouped[rows, g, h].rearrange("k (p s) t -> k p s t", p=O),
-                    in0=core0_raw[rows, g:I:GROUPS, :].rearrange("k t (s p) -> k p s t", p=O),
-                    scalar1=1.0,
-                    scalar2=0.0,
-                    op0=mybir.AluOpType.mult,
-                    op1=mybir.AluOpType.add,
-                )
+            o_ = core0_grouped[rows, g, h].rearrange("k (p s) t -> k p s t", p=O)
+            i_ = core0_raw[rows, g:I:GROUPS, :].rearrange("k t (s p) -> k p s t", p=O)
+            if how == "G":
+                nc.gpsimd.tensor_scalar(out=o_, in0=i_, scalar1=1.0, scalar2=0.0, op0=mybir.AluOpType.mult, op1=mybir.AluOpType.add)
+            elif how == "V":
+                nc.vector.tensor_copy(out=o_, in_=i_)
+            else:
+                nc.scalar.copy(out=o_, in_=i_)
 
-        def lay_out_core1(h):
+        def prep(step):
+            for n, (at, how) in enumerate(PREP):
+                if at == step:
+                    lay_out_core0(n // 2, n % 2, how)
+            for n, (at, how) in enumerate(L1):
+                if at == step:
+                    lay_out_core1(n // 2, n % 2, how)
+
+        prep(-1)
+
+        def lay_out_core1(h, g, how):
             rows = slice(h * R, (h + 1) * R)
-            nc.gpsimd.tensor_scalar(
-                out=core1_grouped[rows, :, h],
-                in0=core1_raw[rows].rearrange("k (g t) n -> k g n t", t=PACK),
-                scalar1=1.0,
-                scalar2=0.0,
-                op0=mybir.AluOpType.mult,
-                op1=mybir.AluOpType.add,
-            )
+            o_ = core1_grouped[rows, g, h]
+            i_ = core1_raw[rows, g * PACK : (g + 1) * PACK].rearrange("k t n -> k n t")
+            if how == "G":
+                nc.gpsimd.tensor_scalar(out=o_, in0=i_, scalar1=1.0, scalar2=0.0, op0=mybir.AluOpType.mult, op1=mybir.AluOpType.add)
+            elif how == "V":
+                nc.vector.tensor_copy(out=o_, in_=i_)
+            else:
+                nc.scalar.copy(out=o_, in_=i_)
 
         def quantise_core0():
             nc.vector.quantize_mx(
@@ -289,64 +337,117 @@ def tile_mpolinear2_pa_t_kernel(tc, t_first, mid_core0, mid_core1, out):
             )
 
         for g in range(GROUPS):
-            for zl in (0, 1) if g == 0 else (1, 0):
+            for zl in range(ZL):
                 transpose_bank(0, g, zl)
-        for step in range(N_UNITS):
-            turn_over(step, 0, 0)
-            turn_over(step, 0, 1)
-            round_mid(step - ROUND_LAG, 0, nc.scalar.copy)
-            first_contraction(step - FIRST_LAG - 1, 1)
-            turn_over(step, 1, 1)
-            turn_over(step, 1, 0)
-            round_mid(step - ROUND_LAG, 1, nc.scalar.copy)
-            quantise_unit(step - QUANTISE_LAG, 0, GROUPS)
-            if step == FIRST_LAG:
+        def q_step(j):
+            return j if j < L0 else j + 1
+
+        def p_step(k):
+            return q_step(k | 1) + 1 + (k & 1)
+
+        def r_step(k):
+            return p_step(k) + RL
+
+        def m_step(u):
+            return r_step(2 * u + 1) + 1
+
+        def g_step(k):
+            ready = m_step(4 * (k // 4) + 2 + k % 4 // 2) + 1
+            return max(m_step(4 * (k // 4) + 2) + 1 + GS * (k % 4), ready)
+
+        def f_step_old(k):
+            return g_step(k) + FL
+
+        def f_step(k):
+            return f_step_old(k)
+
+        for step in range(N_STEPS):
+            turn_over(step // 2, step % 2, 0)
+            for k in range(2 * N_UNITS - 2):
+                if p_step(k) == step:
+                    first_contraction(k // 2, k % 2)
+            for k in range(N_FINAL - HALVES):
+                if g_step(k) == step:
+                    second_contraction(k)
+            turn_over(step // 2, step % 2, 1)
+            for k in range(2 * N_UNITS - 2):
+                if r_step(k) == step:
+                    round_mid(k // 2, k % 2, nc.scalar.copy)
+            for j in range(2 * N_UNITS - 1):
+                if q_step(j) == step:
+                    quantise_unit(j // 2, j % 2)
+                    separate(j // 2 + SEPARATE_AHEAD, j % 2)
+            prep(step)
+            if step == Q0AT:
                 quantise_core0()
-            if step == SECOND_LAG - 1:
+            if step == Q1AT:
                 quantise_core1()
-            quantise_mid(step - MID_LAG)
-            separate(step + SEPARATE_AHEAD, 0)
-            separate(step + SEPARATE_AHEAD, 1)
-            if step in (2, 3):
-                lay_out_core1(step - 2)
-            first_contraction(step - FIRST_LAG, 0)
-            second_contraction(step - SECOND_LAG)
-            finish(step - FINISH_LAG)
+            for u in range(N_UNITS - 1):
+                if m_step(u) == step:
+                    quantise_mid(u)
+            for k in range(N_FINAL - HALVES):
+                if f_step(k) == step:
+                    finish(k)
 
         last, before = N_UNITS - 1, N_UNITS - 2
         bq, zq = N_BQ - 1, ZQ - 1
-        first_contraction(before, 1)
-        quantise_unit(last, 0, 1)
-        quantise_unit(last, 1, 1)
-        for group in range(last - SECOND_LAG + 1, N_FINAL - 2 * HALVES):
-            second_contraction(group)
+        for k in range(2 * last):
+            if p_step(k) >= N_STEPS:
+                first_contraction(k // 2, k % 2)
         for h in range(HALVES):
             accs[last, h] = new_acc(last, h)
             first_pass(accs[last, h], last, h, 0)
+        quantise_unit(last, 1)
+        if TG == 0:
+            for group in range(N_FINAL - 2 * HALVES):
+                if g_step(group) >= N_STEPS:
+                    second_contraction(group)
         for h in range(HALVES):
             first_pass(accs[last, h], last, h, 1)
-        for h in range(HALVES):
-            round_mid(before, h, nc.scalar.copy)
-        for group in range(last - FINISH_LAG + 1, N_FINAL - 2 * HALVES):
-            finish(group)
-        for unit in range(last - MID_LAG + 1, last):
-            quantise_mid(unit)
+        if TG == 1:
+            for group in range(N_FINAL - 2 * HALVES):
+                if g_step(group) >= N_STEPS:
+                    second_contraction(group)
+        for k in range(2 * last):
+            if r_step(k) >= N_STEPS:
+                round_mid(k // 2, k % 2, nc.scalar.copy)
+        for group in range(N_FINAL - 2 * HALVES):
+            if f_step(group) >= N_STEPS:
+                finish(group)
+        for unit in range(last):
+            if m_step(unit) >= N_STEPS:
+                quantise_mid(unit)
         round_mid(last, 0, nc.scalar.copy)
         round_mid(last, 1, nc.vector.tensor_copy)
         for group in range(N_FINAL - 2 * HALVES, N_FINAL - HALVES):
-            second_contraction(group)
-        finish(N_FINAL - HALVES - 1)
-        halves = []
-        for h in range(HALVES):
-            halves.append(psum_t.tile([P, HALVES * N_OUT], F32, name="bank"))
-            second_pass(halves[h][:], bq, 0, zq, h)
-        quantise_mid(last)
-        for h in range(HALVES):
-            second_pass(halves[h][:], bq, 1, zq, h)
-        for h in range(HALVES):
-            result = work.tile([P, 1, HALVES * N_OUT], F32, name="last_result")
-            if h == 0:
-                nc.scalar.copy(out=result[:, 0], in_=halves[h][:])
-            else:
-                nc.vector.tensor_copy(out=result[:, 0], in_=halves[h][:])
-            store(result, bq, zq, h, 1, nc.scalar if h == 0 else nc.sync)
+            if g_step(group) >= N_STEPS:
+                second_contraction(group)
+        if f_step(N_FINAL - HALVES - 1) >= N_STEPS:
+            finish(N_FINAL - HALVES - 1)
+        if LMODE == 0:
+            halves = []
+            for h in range(HALVES):
+                halves.append(psum_t.tile([P, HALVES * N_OUT], F32, name="bank"))
+                second_pass(halves[h][:], bq, 0, zq, h)
+            quantise_mid(last)
+            for h in range(HALVES):
+                second_pass(halves[h][:], bq, 1, zq, h)
+            for h in range(HALVES):
+                result = work.tile([P, 1, HALVES * N_OUT], F32, name="last_result")
+                if h == 0:
+                    nc.scalar.copy(out=result[:, 0], in_=halves[h][:])
+                else:
+                    nc.vector.tensor_copy(out=result[:, 0], in_=halves[h][:])
+                store(result, bq, zq, h, 1, nc.scalar if h == 0 else nc.sync)
+        else:
+            halves = []
+            for h in range(HALVES):
+                halves.append(psum_t.tile([P, HALVES * N_OUT], F32, name="bank"))
+                second_pass(halves[h][:], bq, 0, zq, h)
+            quantise_mid(last)
+            for h in range(HALVES):
+                second_pass(halves[h][:], bq, 1, zq, h)
+            result = work.tile([P, HALVES, HALVES * N_OUT], F32, name="result")
+            nc.scalar.copy(out=result[:, 0], in_=halves[0][:])
+            nc.vector.tensor_copy(out=result[:, 1], in_=halves[1][:])
+            store(result, bq, zq, 0, HALVES, nc.sync)

@@ -12,7 +12,7 @@ FP8X4 = mybir.dt.float8_e4m3fn_x4
 P = 128
 S_EXTRA = ()
 SEP = (5, 7, 9, 11, 13, 15)
-FV = ()
+FV = ((1, 1), (3, 1))
 RV = ()
 GB = 3
 C0AT = 0
@@ -22,7 +22,7 @@ TG = 0
 GS = 1
 LMODE = 1
 SPLIT0 = 0
-Q0AT = 1
+Q0AT = 2
 BANKACC = 28
 PACK = 4
 B, I, R, O = 128, 8, 64, 2
@@ -35,15 +35,15 @@ BANK = 512
 ZQ, ZL = 2, 2
 B_CHUNK = P // PACK
 N_BQ = B // B_CHUNK
-N_HEAD = 6
+N_HEAD = 4
 N_UNITS = N_BQ * GROUPS * ZQ
 N_FINAL = N_BQ * ZQ * HALVES
 
-L0 = 4
-RL = 1
+L0 = 0
+RL = 2
 FL = 1
 Q1AT = 9
-L1 = ((4, 'G'), (4, 'G'), (4, 'G'), (4, 'G'))
+L1 = ((4, 'S'), (4, 'S'), (5, 'S'), (5, 'S'))
 SEPARATE_AHEAD = 2
 N_STEPS = 2 * N_UNITS
 

@@ -22,7 +22,7 @@ TG = 0
 GS = 1
 LMODE = 1
 SPLIT0 = 0
-Q0AT = 2
+Q0AT = 3
 BANKACC = 28
 PACK = 4
 B, I, R, O = 128, 8, 64, 2
@@ -35,14 +35,18 @@ BANK = 512
 ZQ, ZL = 2, 2
 B_CHUNK = P // PACK
 N_BQ = B // B_CHUNK
-N_HEAD = 4
+N_HEAD = 6
 N_UNITS = N_BQ * GROUPS * ZQ
 N_FINAL = N_BQ * ZQ * HALVES
 
 L0 = 0
+QL = 1
+PL = 1
+PLATE = 1
+MFIRST = 1
 RL = 2
-FL = 1
-Q1AT = 9
+FL = 2
+Q1AT = 11
 L1 = ((4, 'S'), (4, 'S'), (5, 'S'), (5, 'S'))
 SEPARATE_AHEAD = 2
 N_STEPS = 2 * N_UNITS
@@ -340,10 +344,10 @@ def tile_mpolinear2_pa_t_kernel(tc, t_first, mid_core0, mid_core1, out):
             for zl in range(ZL):
                 transpose_bank(0, g, zl)
         def q_step(j):
-            return j if j < L0 else j + 1
+            return j if j < L0 else j + QL
 
         def p_step(k):
-            return q_step(k | 1) + 1 + (k & 1)
+            return q_step(k | 1) + PL + (k & 1)
 
         def r_step(k):
             return p_step(k) + RL
@@ -362,13 +366,18 @@ def tile_mpolinear2_pa_t_kernel(tc, t_first, mid_core0, mid_core1, out):
             return f_step_old(k)
 
         for step in range(N_STEPS):
+            if MFIRST:
+                for u in range(N_UNITS - 1):
+                    if m_step(u) == step:
+                        quantise_mid(u)
             turn_over(step // 2, step % 2, 0)
-            for k in range(2 * N_UNITS - 2):
-                if p_step(k) == step:
-                    first_contraction(k // 2, k % 2)
-            for k in range(N_FINAL - HALVES):
-                if g_step(k) == step:
-                    second_contraction(k)
+            if not PLATE:
+                for k in range(2 * N_UNITS - 2):
+                    if p_step(k) == step:
+                        first_contraction(k // 2, k % 2)
+                for k in range(N_FINAL - HALVES):
+                    if g_step(k) == step:
+                        second_contraction(k)
             turn_over(step // 2, step % 2, 1)
             for k in range(2 * N_UNITS - 2):
                 if r_step(k) == step:
@@ -378,12 +387,23 @@ def tile_mpolinear2_pa_t_kernel(tc, t_first, mid_core0, mid_core1, out):
                     quantise_unit(j // 2, j % 2)
                     separate(j // 2 + SEPARATE_AHEAD, j % 2)
             prep(step)
-            if step == Q0AT:
+            if step == Q0AT and PLATE:
                 quantise_core0()
-            if step == Q1AT:
+            if step == Q1AT and PLATE:
+                quantise_core1()
+            if PLATE:
+                for k in range(2 * N_UNITS - 2):
+                    if p_step(k) == step:
+                        first_contraction(k // 2, k % 2)
+                for k in range(N_FINAL - HALVES):
+                    if g_step(k) == step:
+                        second_contraction(k)
+            if step == Q0AT and not PLATE:
+                quantise_core0()
+            if step == Q1AT and not PLATE:
                 quantise_core1()
             for u in range(N_UNITS - 1):
-                if m_step(u) == step:
+                if not MFIRST and m_step(u) == step:
                     quantise_mid(u)
             for k in range(N_FINAL - HALVES):
                 if f_step(k) == step:
@@ -391,9 +411,14 @@ def tile_mpolinear2_pa_t_kernel(tc, t_first, mid_core0, mid_core1, out):
 
         last, before = N_UNITS - 1, N_UNITS - 2
         bq, zq = N_BQ - 1, ZQ - 1
+        for j in range(2 * last):
+            if q_step(j) >= N_STEPS:
+                quantise_unit(j // 2, j % 2)
         for k in range(2 * last):
             if p_step(k) >= N_STEPS:
                 first_contraction(k // 2, k % 2)
+        if q_step(2 * last) >= N_STEPS:
+            quantise_unit(last, 0)
         for h in range(HALVES):
             accs[last, h] = new_acc(last, h)
             first_pass(accs[last, h], last, h, 0)

@@ -10,46 +10,33 @@ U8 = mybir.dt.uint8
 FP8X4 = mybir.dt.float8_e4m3fn_x4
 
 P = 128
-S_EXTRA = ()
-SEP = (5, 7, 9, 11, 13, 15)
-FV = ((1, 1), (3, 1))
-RV = ()
-GB = 3
-C0AT = 0
-C1AT = 2
-PREP = ((-1, 'G'), (-1, 'G'), (-1, 'G'), (-1, 'G'))
-TG = 0
-GS = 1
-LMODE = 1
-SPLIT0 = 0
-Q0AT = 3
-BANKACC = 28
 PACK = 4
 B, I, R, O = 128, 8, 64, 2
 HALVES = P // R
 GROUPS = I // PACK
 N_OUT = R * O
-UNIT_RUN = 4 * R * O
 BANK = 512
 
 ZQ, ZL = 2, 2
+UNIT_RUN = ZL * HALVES * R * O
 B_CHUNK = P // PACK
 N_BQ = B // B_CHUNK
-N_HEAD = 6
 N_UNITS = N_BQ * GROUPS * ZQ
+N_PRODUCTS = N_UNITS * HALVES
 N_FINAL = N_BQ * ZQ * HALVES
-
-L0 = 0
-QL = 1
-PL = 1
-PLATE = 1
-MFIRST = 1
-RL = 2
-FL = 2
-Q1AT = 11
-L1 = ((4, 'S'), (4, 'S'), (5, 'S'), (5, 'S'))
+N_HEAD = 4
+FIRST_SEPARATED = 5
 SEPARATE_AHEAD = 2
-N_STEPS = 2 * N_UNITS
+
+N_STEPS = N_UNITS * GROUPS
+QUANTISE_LAG = 1
+PRODUCT_LAG = 3
+ROUND_LAG = 5
+MID_LAG = 7
+SECOND_LAG = 12
+FINISH_LAG = 15
+
+FILL_BEFORE, FILL_AFTER = 512, 128
 
 FLOPS = 2 * (B * I * I * O) * (I * R) * N_OUT + 2 * (B * I * O * O) * (I * R) * N_OUT
 
@@ -60,38 +47,26 @@ def tile_mpolinear2_pa_t_kernel(tc, t_first, mid_core0, mid_core1, out):
         consts = ctx.enter_context(tc.tile_pool(name="consts", bufs=1))
         raw_pool = ctx.enter_context(tc.tile_pool(name="raw_pool", bufs=(N_UNITS - N_HEAD) // ZQ * GROUPS))
         head_pool = ctx.enter_context(tc.tile_pool(name="head_pool", bufs=N_HEAD * GROUPS))
+        grouped_pool = ctx.enter_context(tc.tile_pool(name="grouped_pool", bufs=SEPARATE_AHEAD + 1))
         work = ctx.enter_context(tc.tile_pool(name="work", bufs=3))
-        grouped_pool = ctx.enter_context(tc.tile_pool(name="grouped_pool", bufs=GB))
         psum_t = ctx.enter_context(tc.psum_pool(name="psum_t", bufs=GROUPS * ZL))
         psum_1 = ctx.enter_context(tc.psum_pool(name="psum_1", bufs=HALVES))
         psum_2 = ctx.enter_context(tc.psum_pool(name="psum_2", bufs=2))
         ctx.enter_context(tc.manual_schedule())
 
-        first_parts = {}
         raw, banks, grouped, codes, scales = {}, {}, {}, {}, {}
         accs, mids, mid_codes, mid_scales, accs2 = {}, {}, {}, {}, {}
 
         def split_unit(unit):
             return unit // (GROUPS * ZQ), unit // ZQ % GROUPS, unit % ZQ
 
+        def split_group(group):
+            return group // (ZQ * HALVES), group // HALVES % ZQ, group % HALVES
+
         def load(unit):
             bq, yg, zq = split_unit(unit)
             for g in range(GROUPS):
-                if unit == 0 and g < SPLIT0:
-                    parts = []
-                    for zl in range(ZL):
-                        tile = head_pool.tile([P, PACK, HALVES * R * O], BF16, name="first_raw")
-                        parts.append(tile)
-                        for y in range(PACK):
-                            nc.sync.dma_start(
-                                out=tile[y:P:PACK],
-                                in_=t_first[
-                                    bq * B_CHUNK : (bq + 1) * B_CHUNK, g:I:GROUPS, yg * PACK + y, zl * HALVES : (zl + 1) * HALVES
-                                ].rearrange("b x z r o -> b x (z r o)"),
-                            )
-                    first_parts[g] = parts
-                    continue
-                elif unit < N_HEAD:
+                if unit < N_HEAD:
                     zqs = slice(zq, zq + 1)
                     tile = head_pool.tile([P, PACK, 1, UNIT_RUN], BF16, name="head_raw")
                     raw[unit, g] = tile[:, :, 0]
@@ -114,23 +89,24 @@ def tile_mpolinear2_pa_t_kernel(tc, t_first, mid_core0, mid_core1, out):
                     )
 
         def is_separated(unit, g, zl):
-            return unit in SEP and g == GROUPS - 1 and zl == ZL - 1
+            return unit >= FIRST_SEPARATED and unit % 2 == 1 and g == GROUPS - 1 and zl == ZL - 1
+
+        def separated(unit, u):
+            older = grouped[unit - SEPARATE_AHEAD][:, u].rearrange("k o z c t -> k (o z c t)")
+            return older[:, : O * P * 2]
 
         def separate(unit, u):
-            if unit >= N_UNITS or unit not in SEP:
+            g, zl = GROUPS - 1, ZL - 1
+            if unit >= N_UNITS or not is_separated(unit, g, zl):
                 return
             nc.gpsimd.tensor_scalar(
                 out=separated(unit, u).rearrange("k (o n e) -> k o n e", o=O, e=2),
-                in0=raw[unit, GROUPS - 1][:, 2 * u : 2 * u + 2, (ZL - 1) * 2 * P :].rearrange("k e (n o) -> k o n e", o=O),
+                in0=raw[unit, g][:, 2 * u : 2 * u + 2, zl * 2 * P :].rearrange("k e (n o) -> k o n e", o=O),
                 scalar1=1.0,
                 scalar2=0.0,
                 op0=mybir.AluOpType.mult,
                 op1=mybir.AluOpType.add,
             )
-
-        def separated(unit, u):
-            older = grouped[unit - SEPARATE_AHEAD][:, u].rearrange("k o z c t -> k (o z c t)")
-            return older[:, : O * P * 2]
 
         def transpose_bank(unit, g, zl):
             if unit >= N_UNITS:
@@ -142,35 +118,30 @@ def tile_mpolinear2_pa_t_kernel(tc, t_first, mid_core0, mid_core1, out):
                     for o in range(O):
                         nc.tensor.transpose(bank[:, 2 * o + u, :], words[:, o * P : (o + 1) * P], ident[:])
             else:
-                if unit == 0 and g in first_parts:
-                    words = first_parts[g][zl][:].bitcast(F32)
-                else:
-                    words = raw[unit, g].bitcast(F32)[:, :, zl * P : (zl + 1) * P]
+                words = raw[unit, g].bitcast(F32)[:, :, zl * P : (zl + 1) * P]
                 for t in range(PACK):
                     nc.tensor.transpose(bank[:, t, :], words[:, t], ident[:])
             banks[unit, g, zl] = bank
 
         def turn_over(unit, g, zl):
-            if unit >= N_UNITS:
-                return
             if g == 0 and zl == 0:
                 grouped[unit] = grouped_pool.tile([P, GROUPS, O, ZL, P, PACK], BF16, name="grouped", align_bytes=64)
-            halves = banks[unit, g, zl][:].bitcast(BF16).rearrange("k t (c o) -> k o c t", o=O)
+            bank = banks[unit, g, zl]
             if is_separated(unit, g, zl):
                 words = grouped[unit][:].rearrange("k g o z c t -> k (g o z c t)").bitcast(F32)
                 words = words.rearrange("k (g o z c u) -> k g o z c u", g=GROUPS, o=O, z=ZL, u=2)
                 nc.vector.tensor_copy(
-                    out=words[:, g, :, zl], in_=banks[unit, g, zl][:].rearrange("k (o u) c -> k o c u", o=O)
+                    out=words[:, g, :, zl], in_=bank[:].rearrange("k (o u) c -> k o c u", o=O)
                 )
-            elif zl == 0 or (unit, g) in S_EXTRA:
-                nc.scalar.copy(out=grouped[unit][:, g, :, zl], in_=halves)
             else:
-                nc.vector.tensor_copy(out=grouped[unit][:, g, :, zl], in_=halves)
+                copy = nc.scalar.copy if zl == 0 else nc.vector.tensor_copy
+                copy(
+                    out=grouped[unit][:, g, :, zl],
+                    in_=bank[:].bitcast(BF16).rearrange("k t (c o) -> k o c t", o=O),
+                )
             transpose_bank(unit + 1, g, zl)
 
-        def quantise_unit(unit, g):
-            if not 0 <= unit < N_UNITS:
-                return
+        def quantise_half_unit(unit, g):
             if g == 0:
                 codes[unit] = work.tile([P, GROUPS, BANK], U32, name="codes", align_bytes=64)
                 scales[unit] = work.tile([P, GROUPS, BANK], U8, name="scales", align_bytes=64)
@@ -180,39 +151,38 @@ def tile_mpolinear2_pa_t_kernel(tc, t_first, mid_core0, mid_core1, out):
                 in_=grouped[unit][:, g].rearrange("k o z c t -> k (o z c t)"),
             )
 
-        def first_pass(acc, unit, h, g):
+        def first_pass(k, g, columns, start, stop):
+            unit, h = k // HALVES, k % HALVES
             nc.tensor.matmul_mx(
-                out=acc[:],
+                out=accs[k][:, :columns],
                 lhsT=core0_codes[:, g, h].bitcast(FP8X4),
                 lhsT_scale=core0_scales[:, g, h],
-                rhs=codes[unit][:, g].bitcast(FP8X4),
-                rhs_scale=scales[unit][:, g],
-                start=(g == 0),
-                stop=(g == GROUPS - 1),
+                rhs=codes[unit][:, g, :columns].bitcast(FP8X4),
+                rhs_scale=scales[unit][:, g, :columns],
+                start=start,
+                stop=stop,
             )
 
-        def new_acc(unit, h):
-            if 2 * unit + h >= BANKACC:
-                return psum_t.tile([P, BANK], F32, name="bank")
-            return psum_1.tile([P, BANK], F32, name="acc")
+        def new_acc(k):
+            if k + PRODUCT_LAG >= N_STEPS - 1:
+                accs[k] = psum_t.tile([P, BANK], F32, name="bank")
+            else:
+                accs[k] = psum_1.tile([P, BANK], F32, name="acc")
 
-        def first_contraction(unit, h):
-            if unit < 0:
-                return
-            accs[unit, h] = new_acc(unit, h)
+        def first_contraction(k):
+            new_acc(k)
+            fill = FILL_BEFORE if k + PRODUCT_LAG < SECOND_LAG else FILL_AFTER
+            first_pass(k, 0, fill, start=True, stop=True)
             for g in range(GROUPS):
-                first_pass(accs[unit, h], unit, h, g)
+                first_pass(k, g, BANK, start=(g == 0), stop=(g == GROUPS - 1))
 
-        def round_mid(unit, h, copy):
-            if unit < 0:
-                return
+        def round_mid(k, copy):
+            unit, h = k // HALVES, k % HALVES
             if h == 0:
                 mids[unit] = work.tile([P, HALVES, BANK], BF16, name="mid", align_bytes=64)
-            (nc.vector.tensor_copy if (unit, h) in RV else copy)(out=mids[unit][:, h], in_=accs[unit, h][:])
+            copy(out=mids[unit][:, h], in_=accs[k][:])
 
         def quantise_mid(unit):
-            if unit < 0:
-                return
             bq, yg, zq = split_unit(unit)
             if yg == 0 and zq == 0:
                 mid_codes[bq] = work.tile([P, GROUPS, ZQ, HALVES, P], U32, name="mid_codes", align_bytes=64)
@@ -223,7 +193,8 @@ def tile_mpolinear2_pa_t_kernel(tc, t_first, mid_core0, mid_core1, out):
                 in_=mids[unit][:].rearrange("k h n -> k (h n)"),
             )
 
-        def second_pass(acc2, bq, yg, zq, h):
+        def second_pass(acc2, group, yg):
+            bq, zq, h = split_group(group)
             nc.tensor.matmul_mx(
                 out=acc2,
                 lhsT=mid_codes[bq][:, yg, zq, h].bitcast(FP8X4),
@@ -234,36 +205,32 @@ def tile_mpolinear2_pa_t_kernel(tc, t_first, mid_core0, mid_core1, out):
                 stop=(yg == GROUPS - 1),
             )
 
-        def split_group(group):
-            return group // (ZQ * HALVES), group // HALVES % ZQ, group % HALVES
-
-        def second_contraction(group):
-            if group < 0:
-                return
+        def second_contraction(n):
+            group, yg = n // GROUPS, n % GROUPS
             bq, zq, h = split_group(group)
-            if h == 0:
+            if h == 0 and yg == 0:
                 accs2[bq, zq] = psum_2.tile([P, HALVES, HALVES * N_OUT], F32, name="acc2")
-            for yg in range(GROUPS):
-                second_pass(accs2[bq, zq][:, h], bq, yg, zq, h)
+            second_pass(accs2[bq, zq][:, h], group, yg)
 
-        def store(result, bq, zq, h_first, n_h, queue):
+        def store(result, bq, zq):
             for o in range(O):
                 for zl in range(ZL):
                     first = (o * ZL + zl) * B_CHUNK
-                    z = (zq * ZL + zl) * HALVES + h_first
-                    queue.dma_start(
-                        out=out[bq * B_CHUNK : (bq + 1) * B_CHUNK, z : z + n_h, o].rearrange("b z p u q -> b z (p u q)"),
+                    z = (zq * ZL + zl) * HALVES
+                    nc.sync.dma_start(
+                        out=out[bq * B_CHUNK : (bq + 1) * B_CHUNK, z : z + HALVES, o].rearrange(
+                            "b z p u q -> b z (p u q)"
+                        ),
                         in_=result[first : first + B_CHUNK],
                     )
 
         def finish(group):
-            if group < 0 or group % HALVES != HALVES - 1:
+            bq, zq, h = split_group(group)
+            if h != HALVES - 1:
                 return
-            bq, zq = split_group(group)[:2]
             result = work.tile([P, HALVES, HALVES * N_OUT], F32, name="result")
-            copy = nc.vector.tensor_copy if (bq, zq) in FV else nc.scalar.copy
-            copy(out=result[:], in_=accs2[bq, zq][:])
-            store(result, bq, zq, 0, HALVES, nc.sync)
+            nc.scalar.copy(out=result[:], in_=accs2[bq, zq][:])
+            store(result, bq, zq)
 
         core0_raw = consts.tile([P, I, N_OUT], BF16, name="core0_raw")
         core1_raw = consts.tile([P, I, N_OUT], BF16, name="core1_raw")
@@ -283,48 +250,26 @@ def tile_mpolinear2_pa_t_kernel(tc, t_first, mid_core0, mid_core1, out):
         nc.gpsimd.memset(core0_grouped[:].rearrange("k g h n t -> k (g h n t)").bitcast(F32), 0.0)
         nc.gpsimd.memset(core1_grouped[:].rearrange("k g h n t -> k (g h n t)").bitcast(F32), 0.0)
 
-        def load_core(raw_core, core):
+        def half(h):
+            return slice(h * R, (h + 1) * R)
+
+        def load_core(core_raw, core_rows):
             for h in range(HALVES):
-                nc.sync.dma_start(out=raw_core[h * R : (h + 1) * R], in_=core)
+                nc.sync.dma_start(out=core_raw[half(h)], in_=core_rows)
 
-        for unit in range(N_UNITS):
-            load(unit)
-            if unit == C0AT:
-                load_core(core0_raw, mid_core0.rearrange("x r s p -> r x (s p)"))
-            if unit == C1AT:
-                load_core(core1_raw, mid_core1.rearrange("y s u q -> s y (u q)"))
+        def lay_out_core0(h, copy):
+            for g in range(GROUPS):
+                copy(
+                    out=core0_grouped[half(h), g, h].rearrange("k (p s) t -> k p s t", p=O),
+                    in_=core0_raw[half(h), g:I:GROUPS, :].rearrange("k t (s p) -> k p s t", p=O),
+                )
 
-        def lay_out_core0(h, g, how):
-            rows = slice(h * R, (h + 1) * R)
-            o_ = core0_grouped[rows, g, h].rearrange("k (p s) t -> k p s t", p=O)
-            i_ = core0_raw[rows, g:I:GROUPS, :].rearrange("k t (s p) -> k p s t", p=O)
-            if how == "G":
-                nc.gpsimd.tensor_scalar(out=o_, in0=i_, scalar1=1.0, scalar2=0.0, op0=mybir.AluOpType.mult, op1=mybir.AluOpType.add)
-            elif how == "V":
-                nc.vector.tensor_copy(out=o_, in_=i_)
-            else:
-                nc.scalar.copy(out=o_, in_=i_)
-
-        def prep(step):
-            for n, (at, how) in enumerate(PREP):
-                if at == step:
-                    lay_out_core0(n // 2, n % 2, how)
-            for n, (at, how) in enumerate(L1):
-                if at == step:
-                    lay_out_core1(n // 2, n % 2, how)
-
-        prep(-1)
-
-        def lay_out_core1(h, g, how):
-            rows = slice(h * R, (h + 1) * R)
-            o_ = core1_grouped[rows, g, h]
-            i_ = core1_raw[rows, g * PACK : (g + 1) * PACK].rearrange("k t n -> k n t")
-            if how == "G":
-                nc.gpsimd.tensor_scalar(out=o_, in0=i_, scalar1=1.0, scalar2=0.0, op0=mybir.AluOpType.mult, op1=mybir.AluOpType.add)
-            elif how == "V":
-                nc.vector.tensor_copy(out=o_, in_=i_)
-            else:
-                nc.scalar.copy(out=o_, in_=i_)
+        def lay_out_core1(h):
+            for g in range(GROUPS):
+                nc.scalar.copy(
+                    out=core1_grouped[half(h), g, h],
+                    in_=core1_raw[half(h), g * PACK : (g + 1) * PACK].rearrange("k t n -> k n t"),
+                )
 
         def quantise_core0():
             nc.vector.quantize_mx(
@@ -340,139 +285,76 @@ def tile_mpolinear2_pa_t_kernel(tc, t_first, mid_core0, mid_core1, out):
                 in_=core1_grouped[:].rearrange("k g h n t -> k (g h n t)"),
             )
 
+        for unit in range(N_UNITS):
+            load(unit)
+            if unit == 0:
+                load_core(core0_raw, mid_core0.rearrange("x r s p -> r x (s p)"))
+            if unit == 2:
+                load_core(core1_raw, mid_core1.rearrange("y s u q -> s y (u q)"))
+
         for g in range(GROUPS):
             for zl in range(ZL):
                 transpose_bank(0, g, zl)
-        def q_step(j):
-            return j if j < L0 else j + QL
-
-        def p_step(k):
-            return q_step(k | 1) + PL + (k & 1)
-
-        def r_step(k):
-            return p_step(k) + RL
-
-        def m_step(u):
-            return r_step(2 * u + 1) + 1
-
-        def g_step(k):
-            ready = m_step(4 * (k // 4) + 2 + k % 4 // 2) + 1
-            return max(m_step(4 * (k // 4) + 2) + 1 + GS * (k % 4), ready)
-
-        def f_step_old(k):
-            return g_step(k) + FL
-
-        def f_step(k):
-            return f_step_old(k)
-
         for step in range(N_STEPS):
-            if MFIRST:
-                for u in range(N_UNITS - 1):
-                    if m_step(u) == step:
-                        quantise_mid(u)
-            turn_over(step // 2, step % 2, 0)
-            if not PLATE:
-                for k in range(2 * N_UNITS - 2):
-                    if p_step(k) == step:
-                        first_contraction(k // 2, k % 2)
-                for k in range(N_FINAL - HALVES):
-                    if g_step(k) == step:
-                        second_contraction(k)
-            turn_over(step // 2, step % 2, 1)
-            for k in range(2 * N_UNITS - 2):
-                if r_step(k) == step:
-                    round_mid(k // 2, k % 2, nc.scalar.copy)
-            for j in range(2 * N_UNITS - 1):
-                if q_step(j) == step:
-                    quantise_unit(j // 2, j % 2)
-                    separate(j // 2 + SEPARATE_AHEAD, j % 2)
-            prep(step)
-            if step == Q0AT and PLATE:
+            if step >= MID_LAG and (step - MID_LAG) % GROUPS == 0:
+                quantise_mid((step - MID_LAG) // GROUPS)
+            for zl in range(ZL):
+                turn_over(step // GROUPS, step % GROUPS, zl)
+            if step >= ROUND_LAG:
+                round_mid(step - ROUND_LAG, nc.scalar.copy)
+            if step >= QUANTISE_LAG:
+                unit, g = (step - QUANTISE_LAG) // GROUPS, (step - QUANTISE_LAG) % GROUPS
+                quantise_half_unit(unit, g)
+                separate(unit + SEPARATE_AHEAD, g)
+            if step == 1:
+                lay_out_core0(0, nc.vector.tensor_copy)
+                lay_out_core0(1, nc.scalar.copy)
+            if step == 4 or step == 5:
+                lay_out_core1(step - 4)
+            if step == PRODUCT_LAG:
                 quantise_core0()
-            if step == Q1AT and PLATE:
+            if step == SECOND_LAG - 1:
                 quantise_core1()
-            if PLATE:
-                for k in range(2 * N_UNITS - 2):
-                    if p_step(k) == step:
-                        first_contraction(k // 2, k % 2)
-                for k in range(N_FINAL - HALVES):
-                    if g_step(k) == step:
-                        second_contraction(k)
-            if step == Q0AT and not PLATE:
-                quantise_core0()
-            if step == Q1AT and not PLATE:
-                quantise_core1()
-            for u in range(N_UNITS - 1):
-                if not MFIRST and m_step(u) == step:
-                    quantise_mid(u)
-            for k in range(N_FINAL - HALVES):
-                if f_step(k) == step:
-                    finish(k)
+            if step >= PRODUCT_LAG:
+                first_contraction(step - PRODUCT_LAG)
+            if step >= SECOND_LAG:
+                second_contraction(step - SECOND_LAG)
+            if step >= FINISH_LAG and (step - FINISH_LAG) % 2 == 0:
+                finish((step - FINISH_LAG) // 2)
 
-        last, before = N_UNITS - 1, N_UNITS - 2
-        bq, zq = N_BQ - 1, ZQ - 1
-        for j in range(2 * last):
-            if q_step(j) >= N_STEPS:
-                quantise_unit(j // 2, j % 2)
-        for k in range(2 * last):
-            if p_step(k) >= N_STEPS:
-                first_contraction(k // 2, k % 2)
-        if q_step(2 * last) >= N_STEPS:
-            quantise_unit(last, 0)
+        last = N_UNITS - 1
+        last_products = [last * HALVES + h for h in range(HALVES)]
+        last_groups = [N_FINAL - HALVES + h for h in range(HALVES)]
+        for k in range(N_STEPS - PRODUCT_LAG, N_PRODUCTS - HALVES):
+            first_contraction(k)
+        for k in last_products:
+            new_acc(k)
+            first_pass(k, 0, BANK, start=True, stop=False)
+        quantise_half_unit(last, GROUPS - 1)
+        older_passes = (N_FINAL - 2 * HALVES) * GROUPS
+        for n in range(N_STEPS - SECOND_LAG, older_passes):
+            second_contraction(n)
+        for k in last_products:
+            first_pass(k, GROUPS - 1, BANK, start=False, stop=True)
+        for k in range(N_STEPS - ROUND_LAG, N_PRODUCTS - HALVES):
+            round_mid(k, nc.scalar.copy)
+        for group in range((N_STEPS - FINISH_LAG) // 2 + 1, N_FINAL - 2 * HALVES):
+            finish(group)
+        for unit in range((N_STEPS - MID_LAG) // GROUPS + 1, last):
+            quantise_mid(unit)
+        round_mid(last_products[0], nc.scalar.copy)
+        round_mid(last_products[1], nc.vector.tensor_copy)
+        for n in range(older_passes, (N_FINAL - HALVES) * GROUPS):
+            second_contraction(n)
+        finish(N_FINAL - HALVES - 1)
+        sums = []
+        for group in last_groups:
+            sums.append(psum_t.tile([P, HALVES * N_OUT], F32, name="bank"))
+            second_pass(sums[-1][:], group, 0)
+        quantise_mid(last)
         for h in range(HALVES):
-            accs[last, h] = new_acc(last, h)
-            first_pass(accs[last, h], last, h, 0)
-        quantise_unit(last, 1)
-        if TG == 0:
-            for group in range(N_FINAL - 2 * HALVES):
-                if g_step(group) >= N_STEPS:
-                    second_contraction(group)
-        for h in range(HALVES):
-            first_pass(accs[last, h], last, h, 1)
-        if TG == 1:
-            for group in range(N_FINAL - 2 * HALVES):
-                if g_step(group) >= N_STEPS:
-                    second_contraction(group)
-        for k in range(2 * last):
-            if r_step(k) >= N_STEPS:
-                round_mid(k // 2, k % 2, nc.scalar.copy)
-        for group in range(N_FINAL - 2 * HALVES):
-            if f_step(group) >= N_STEPS:
-                finish(group)
-        for unit in range(last):
-            if m_step(unit) >= N_STEPS:
-                quantise_mid(unit)
-        round_mid(last, 0, nc.scalar.copy)
-        round_mid(last, 1, nc.vector.tensor_copy)
-        for group in range(N_FINAL - 2 * HALVES, N_FINAL - HALVES):
-            if g_step(group) >= N_STEPS:
-                second_contraction(group)
-        if f_step(N_FINAL - HALVES - 1) >= N_STEPS:
-            finish(N_FINAL - HALVES - 1)
-        if LMODE == 0:
-            halves = []
-            for h in range(HALVES):
-                halves.append(psum_t.tile([P, HALVES * N_OUT], F32, name="bank"))
-                second_pass(halves[h][:], bq, 0, zq, h)
-            quantise_mid(last)
-            for h in range(HALVES):
-                second_pass(halves[h][:], bq, 1, zq, h)
-            for h in range(HALVES):
-                result = work.tile([P, 1, HALVES * N_OUT], F32, name="last_result")
-                if h == 0:
-                    nc.scalar.copy(out=result[:, 0], in_=halves[h][:])
-                else:
-                    nc.vector.tensor_copy(out=result[:, 0], in_=halves[h][:])
-                store(result, bq, zq, h, 1, nc.scalar if h == 0 else nc.sync)
-        else:
-            halves = []
-            for h in range(HALVES):
-                halves.append(psum_t.tile([P, HALVES * N_OUT], F32, name="bank"))
-                second_pass(halves[h][:], bq, 0, zq, h)
-            quantise_mid(last)
-            for h in range(HALVES):
-                second_pass(halves[h][:], bq, 1, zq, h)
-            result = work.tile([P, HALVES, HALVES * N_OUT], F32, name="result")
-            nc.scalar.copy(out=result[:, 0], in_=halves[0][:])
-            nc.vector.tensor_copy(out=result[:, 1], in_=halves[1][:])
-            store(result, bq, zq, 0, HALVES, nc.sync)
+            second_pass(sums[h][:], last_groups[h], 1)
+        last_result = work.tile([P, HALVES, HALVES * N_OUT], F32, name="last_result")
+        nc.scalar.copy(out=last_result[:, 0], in_=sums[0][:])
+        nc.vector.tensor_copy(out=last_result[:, 1], in_=sums[1][:])
+        store(last_result, N_BQ - 1, ZQ - 1)

from contextlib import ExitStack

import concourse.mybir as mybir
from concourse.masks import make_identity

BF16 = mybir.dt.bfloat16
F32 = mybir.dt.float32
U32 = mybir.dt.uint32
U8 = mybir.dt.uint8
FP8X4 = mybir.dt.float8_e4m3fn_x4

P = 128
PACK = 4
B, I, R, O = 128, 8, 64, 2
HALVES = P // R
GROUPS = I // PACK
N_OUT = R * O
BANK = 512

ZQ, ZL = 2, 2
UNIT_RUN = ZL * HALVES * R * O
B_CHUNK = P // PACK
N_BQ = B // B_CHUNK
N_UNITS = N_BQ * GROUPS * ZQ
N_PRODUCTS = N_UNITS * HALVES
N_FINAL = N_BQ * ZQ * HALVES
N_HEAD = 4
FIRST_SEPARATED = 5
SEPARATE_AHEAD = 2

N_STEPS = N_UNITS * GROUPS
QUANTISE_LAG = 1
PRODUCT_LAG = 3
ROUND_LAG = 5
MID_LAG = 7
SECOND_LAG = 12
FINISH_LAG = 15

FILL_BEFORE, FILL_AFTER = 512, 128

FLOPS = 2 * (B * I * I * O) * (I * R) * N_OUT + 2 * (B * I * O * O) * (I * R) * N_OUT


def tile_mpolinear2_pa_t_kernel(tc, t_first, mid_core0, mid_core1, out):
    nc = tc.nc
    with ExitStack() as ctx:
        consts = ctx.enter_context(tc.tile_pool(name="consts", bufs=1))
        raw_pool = ctx.enter_context(tc.tile_pool(name="raw_pool", bufs=(N_UNITS - N_HEAD) // ZQ * GROUPS))
        head_pool = ctx.enter_context(tc.tile_pool(name="head_pool", bufs=N_HEAD * GROUPS))
        grouped_pool = ctx.enter_context(tc.tile_pool(name="grouped_pool", bufs=SEPARATE_AHEAD + 1))
        work = ctx.enter_context(tc.tile_pool(name="work", bufs=3))
        psum_t = ctx.enter_context(tc.psum_pool(name="psum_t", bufs=GROUPS * ZL))
        psum_1 = ctx.enter_context(tc.psum_pool(name="psum_1", bufs=HALVES))
        psum_2 = ctx.enter_context(tc.psum_pool(name="psum_2", bufs=2))
        ctx.enter_context(tc.manual_schedule())

        raw, banks, grouped, codes, scales = {}, {}, {}, {}, {}
        accs, mids, mid_codes, mid_scales, accs2 = {}, {}, {}, {}, {}

        def split_unit(unit):
            return unit // (GROUPS * ZQ), unit // ZQ % GROUPS, unit % ZQ

        def split_group(group):
            return group // (ZQ * HALVES), group // HALVES % ZQ, group % HALVES

        def load(unit):
            bq, yg, zq = split_unit(unit)
            for g in range(GROUPS):
                if unit < N_HEAD:
                    zqs = slice(zq, zq + 1)
                    tile = head_pool.tile([P, PACK, 1, UNIT_RUN], BF16, name="head_raw")
                    raw[unit, g] = tile[:, :, 0]
                elif zq == 0:
                    zqs = slice(0, ZQ)
                    tile = raw_pool.tile([P, PACK, ZQ, UNIT_RUN], BF16, name="raw")
                    for q in range(ZQ):
                        raw[unit + q, g] = tile[:, :, q]
                else:
                    continue
                for y in range(PACK):
                    nc.sync.dma_start(
                        out=tile[y:P:PACK].rearrange("k x q n -> k x (q n)"),
                        in_=t_first[
                            bq * B_CHUNK : (bq + 1) * B_CHUNK,
                            g:I:GROUPS,
                            yg * PACK + y,
                            zqs.start * ZL * HALVES : zqs.stop * ZL * HALVES,
                        ].rearrange("b x z r o -> b x (z r o)"),
                    )

        def is_separated(unit, g, zl):
            return unit >= FIRST_SEPARATED and unit % 2 == 1 and g == GROUPS - 1 and zl == ZL - 1

        def separated(unit, u):
            older = grouped[unit - SEPARATE_AHEAD][:, u].rearrange("k o z c t -> k (o z c t)")
            return older[:, : O * P * 2]

        def separate(unit, u):
            g, zl = GROUPS - 1, ZL - 1
            if unit >= N_UNITS or not is_separated(unit, g, zl):
                return
            nc.gpsimd.tensor_scalar(
                out=separated(unit, u).rearrange("k (o n e) -> k o n e", o=O, e=2),
                in0=raw[unit, g][:, 2 * u : 2 * u + 2, zl * 2 * P :].rearrange("k e (n o) -> k o n e", o=O),
                scalar1=1.0,
                scalar2=0.0,
                op0=mybir.AluOpType.mult,
                op1=mybir.AluOpType.add,
            )

        def transpose_bank(unit, g, zl):
            if unit >= N_UNITS:
                return
            bank = psum_t.tile([P, PACK, P], F32, name="bank")
            if is_separated(unit, g, zl):
                for u in range(2):
                    words = separated(unit, u).bitcast(F32)
                    for o in range(O):
                        nc.tensor.transpose(bank[:, 2 * o + u, :], words[:, o * P : (o + 1) * P], ident[:])
            else:
                words = raw[unit, g].bitcast(F32)[:, :, zl * P : (zl + 1) * P]
                for t in range(PACK):
                    nc.tensor.transpose(bank[:, t, :], words[:, t], ident[:])
            banks[unit, g, zl] = bank

        def turn_over(unit, g, zl):
            if g == 0 and zl == 0:
                grouped[unit] = grouped_pool.tile([P, GROUPS, O, ZL, P, PACK], BF16, name="grouped", align_bytes=64)
            bank = banks[unit, g, zl]
            if is_separated(unit, g, zl):
                words = grouped[unit][:].rearrange("k g o z c t -> k (g o z c t)").bitcast(F32)
                words = words.rearrange("k (g o z c u) -> k g o z c u", g=GROUPS, o=O, z=ZL, u=2)
                nc.vector.tensor_copy(
                    out=words[:, g, :, zl], in_=bank[:].rearrange("k (o u) c -> k o c u", o=O)
                )
            else:
                copy = nc.scalar.copy if zl == 0 else nc.vector.tensor_copy
                copy(
                    out=grouped[unit][:, g, :, zl],
                    in_=bank[:].bitcast(BF16).rearrange("k t (c o) -> k o c t", o=O),
                )
            transpose_bank(unit + 1, g, zl)

        def quantise_half_unit(unit, g):
            if g == 0:
                codes[unit] = work.tile([P, GROUPS, BANK], U32, name="codes", align_bytes=64)
                scales[unit] = work.tile([P, GROUPS, BANK], U8, name="scales", align_bytes=64)
            nc.vector.quantize_mx(
                out=codes[unit][:, g].bitcast(FP8X4),
                scales=scales[unit][:, g],
                in_=grouped[unit][:, g].rearrange("k o z c t -> k (o z c t)"),
            )

        def first_pass(k, g, columns, start, stop):
            unit, h = k // HALVES, k % HALVES
            nc.tensor.matmul_mx(
                out=accs[k][:, :columns],
                lhsT=core0_codes[:, g, h].bitcast(FP8X4),
                lhsT_scale=core0_scales[:, g, h],
                rhs=codes[unit][:, g, :columns].bitcast(FP8X4),
                rhs_scale=scales[unit][:, g, :columns],
                start=start,
                stop=stop,
            )

        def new_acc(k):
            if k + PRODUCT_LAG >= N_STEPS - 1:
                accs[k] = psum_t.tile([P, BANK], F32, name="bank")
            else:
                accs[k] = psum_1.tile([P, BANK], F32, name="acc")

        def first_contraction(k):
            new_acc(k)
            fill = FILL_BEFORE if k + PRODUCT_LAG < SECOND_LAG else FILL_AFTER
            first_pass(k, 0, fill, start=True, stop=True)
            for g in range(GROUPS):
                first_pass(k, g, BANK, start=(g == 0), stop=(g == GROUPS - 1))

        def round_mid(k, copy):
            unit, h = k // HALVES, k % HALVES
            if h == 0:
                mids[unit] = work.tile([P, HALVES, BANK], BF16, name="mid", align_bytes=64)
            copy(out=mids[unit][:, h], in_=accs[k][:])

        def quantise_mid(unit):
            bq, yg, zq = split_unit(unit)
            if yg == 0 and zq == 0:
                mid_codes[bq] = work.tile([P, GROUPS, ZQ, HALVES, P], U32, name="mid_codes", align_bytes=64)
                mid_scales[bq] = work.tile([P, GROUPS, ZQ, HALVES, P], U8, name="mid_scales", align_bytes=64)
            nc.vector.quantize_mx(
                out=mid_codes[bq][:, yg, zq].rearrange("k h c -> k (h c)").bitcast(FP8X4),
                scales=mid_scales[bq][:, yg, zq].rearrange("k h c -> k (h c)"),
                in_=mids[unit][:].rearrange("k h n -> k (h n)"),
            )

        def second_pass(acc2, group, yg):
            bq, zq, h = split_group(group)
            nc.tensor.matmul_mx(
                out=acc2,
                lhsT=mid_codes[bq][:, yg, zq, h].bitcast(FP8X4),
                lhsT_scale=mid_scales[bq][:, yg, zq, h],
                rhs=core1_codes[:, yg].bitcast(FP8X4),
                rhs_scale=core1_scales[:, yg],
                start=(yg == 0),
                stop=(yg == GROUPS - 1),
            )

        def second_contraction(n):
            group, yg = n // GROUPS, n % GROUPS
            bq, zq, h = split_group(group)
            if h == 0 and yg == 0:
                accs2[bq, zq] = psum_2.tile([P, HALVES, HALVES * N_OUT], F32, name="acc2")
            second_pass(accs2[bq, zq][:, h], group, yg)

        def store(result, bq, zq):
            for o in range(O):
                for zl in range(ZL):
                    first = (o * ZL + zl) * B_CHUNK
                    z = (zq * ZL + zl) * HALVES
                    nc.sync.dma_start(
                        out=out[bq * B_CHUNK : (bq + 1) * B_CHUNK, z : z + HALVES, o].rearrange(
                            "b z p u q -> b z (p u q)"
                        ),
                        in_=result[first : first + B_CHUNK],
                    )

        def finish(group):
            bq, zq, h = split_group(group)
            if h != HALVES - 1:
                return
            result = work.tile([P, HALVES, HALVES * N_OUT], F32, name="result")
            nc.scalar.copy(out=result[:], in_=accs2[bq, zq][:])
            store(result, bq, zq)

        core0_raw = consts.tile([P, I, N_OUT], BF16, name="core0_raw")
        core1_raw = consts.tile([P, I, N_OUT], BF16, name="core1_raw")
        core0_grouped = consts.tile([P, GROUPS, HALVES, N_OUT, PACK], BF16, name="core0_grouped", align_bytes=64)
        core1_grouped = consts.tile([P, GROUPS, HALVES, N_OUT, PACK], BF16, name="core1_grouped", align_bytes=64)
        core0_codes = consts.tile([P, GROUPS, HALVES, N_OUT], U32, name="core0_codes", align_bytes=64)
        core0_scales = consts.tile([P, GROUPS, HALVES, N_OUT], U8, name="core0_scales", align_bytes=64)
        core1_codes = consts.tile([P, GROUPS, HALVES * N_OUT], U32, name="core1_codes", align_bytes=64)
        core1_scales = consts.tile([P, GROUPS, HALVES * N_OUT], U8, name="core1_scales", align_bytes=64)

        spark = consts.tile([P, 2], F32, name="spark")
        nc.vector.memset(spark[:], 0.0)
        nc.scalar.copy(out=spark[:, 1:2], in_=spark[:, 0:1])

        ident = consts.tile([P, P], F32, name="ident")
        make_identity(nc, ident[:])
        nc.gpsimd.memset(core0_grouped[:].rearrange("k g h n t -> k (g h n t)").bitcast(F32), 0.0)
        nc.gpsimd.memset(core1_grouped[:].rearrange("k g h n t -> k (g h n t)").bitcast(F32), 0.0)

        def half(h):
            return slice(h * R, (h + 1) * R)

        def load_core(core_raw, core_rows):
            for h in range(HALVES):
                nc.sync.dma_start(out=core_raw[half(h)], in_=core_rows)

        def lay_out_core0(h, copy):
            for g in range(GROUPS):
                copy(
                    out=core0_grouped[half(h), g, h].rearrange("k (p s) t -> k p s t", p=O),
                    in_=core0_raw[half(h), g:I:GROUPS, :].rearrange("k t (s p) -> k p s t", p=O),
                )

        def lay_out_core1(h):
            for g in range(GROUPS):
                nc.scalar.copy(
                    out=core1_grouped[half(h), g, h],
                    in_=core1_raw[half(h), g * PACK : (g + 1) * PACK].rearrange("k t n -> k n t"),
                )

        def quantise_core0():
            nc.vector.quantize_mx(
                out=core0_codes[:].rearrange("k g h m -> k (g h m)").bitcast(FP8X4),
                scales=core0_scales[:].rearrange("k g h m -> k (g h m)"),
                in_=core0_grouped[:].rearrange("k g h m t -> k (g h m t)"),
            )

        def quantise_core1():
            nc.vector.quantize_mx(
                out=core1_codes[:].rearrange("k g n -> k (g n)").bitcast(FP8X4),
                scales=core1_scales[:].rearrange("k g n -> k (g n)"),
                in_=core1_grouped[:].rearrange("k g h n t -> k (g h n t)"),
            )

        for unit in range(N_UNITS):
            load(unit)
            if unit == 0:
                load_core(core0_raw, mid_core0.rearrange("x r s p -> r x (s p)"))
            if unit == 2:
                load_core(core1_raw, mid_core1.rearrange("y s u q -> s y (u q)"))

        for g in range(GROUPS):
            for zl in range(ZL):
                transpose_bank(0, g, zl)
        for step in range(N_STEPS):
            if step >= MID_LAG and (step - MID_LAG) % GROUPS == 0:
                quantise_mid((step - MID_LAG) // GROUPS)
            for zl in range(ZL):
                turn_over(step // GROUPS, step % GROUPS, zl)
            if step >= ROUND_LAG:
                round_mid(step - ROUND_LAG, nc.scalar.copy)
            if step >= QUANTISE_LAG:
                unit, g = (step - QUANTISE_LAG) // GROUPS, (step - QUANTISE_LAG) % GROUPS
                quantise_half_unit(unit, g)
                separate(unit + SEPARATE_AHEAD, g)
            if step == 1:
                lay_out_core0(0, nc.vector.tensor_copy)
                lay_out_core0(1, nc.scalar.copy)
            if step == 4 or step == 5:
                lay_out_core1(step - 4)
            if step == PRODUCT_LAG:
                quantise_core0()
            if step == SECOND_LAG - 1:
                quantise_core1()
            if step >= PRODUCT_LAG:
                first_contraction(step - PRODUCT_LAG)
            if step >= SECOND_LAG:
                second_contraction(step - SECOND_LAG)
            if step >= FINISH_LAG and (step - FINISH_LAG) % 2 == 0:
                finish((step - FINISH_LAG) // 2)

        last = N_UNITS - 1
        last_products = [last * HALVES + h for h in range(HALVES)]
        last_groups = [N_FINAL - HALVES + h for h in range(HALVES)]
        for k in range(N_STEPS - PRODUCT_LAG, N_PRODUCTS - HALVES):
            first_contraction(k)
        for k in last_products:
            new_acc(k)
            first_pass(k, 0, BANK, start=True, stop=False)
        quantise_half_unit(last, GROUPS - 1)
        older_passes = (N_FINAL - 2 * HALVES) * GROUPS
        for n in range(N_STEPS - SECOND_LAG, older_passes):
            second_contraction(n)
        for k in last_products:
            first_pass(k, GROUPS - 1, BANK, start=False, stop=True)
        for k in range(N_STEPS - ROUND_LAG, N_PRODUCTS - HALVES):
            round_mid(k, nc.scalar.copy)
        for group in range((N_STEPS - FINISH_LAG) // 2 + 1, N_FINAL - 2 * HALVES):
            finish(group)
        for unit in range((N_STEPS - MID_LAG) // GROUPS + 1, last):
            quantise_mid(unit)
        round_mid(last_products[0], nc.scalar.copy)
        round_mid(last_products[1], nc.vector.tensor_copy)
        for n in range(older_passes, (N_FINAL - HALVES) * GROUPS):
            second_contraction(n)
        finish(N_FINAL - HALVES - 1)
        sums = []
        for group in last_groups:
            sums.append(psum_t.tile([P, HALVES * N_OUT], F32, name="bank"))
            second_pass(sums[-1][:], group, 0)
        quantise_mid(last)
        for h in range(HALVES):
            second_pass(sums[h][:], last_groups[h], 1)
        last_result = work.tile([P, HALVES, HALVES * N_OUT], F32, name="last_result")
        nc.scalar.copy(out=last_result[:, 0], in_=sums[0][:])
        nc.vector.tensor_copy(out=last_result[:, 1], in_=sums[1][:])
        store(last_result, N_BQ - 1, ZQ - 1)
